import numpy as np
import ml_dtypes


def mxq(x, axis, fmt="e4m3"):
    dtype, down = {"e4m3": (ml_dtypes.float8_e4m3fn, 7), "e5m2": (ml_dtypes.float8_e5m2, 14)}[fmt]
    v = np.moveaxis(np.asarray(x, np.float32).astype(ml_dtypes.bfloat16).astype(np.float64), axis, -1)
    blocks = v.reshape(v.shape[:-1] + (-1, 32))
    amax = np.abs(blocks).max(-1, keepdims=True)
    byte = np.maximum(np.where(amax > 0, np.frexp(amax)[1] - 1 + 127, 0) - down, 1)
    scale = np.exp2(byte - 127.0)
    codes = (blocks / scale).astype(np.float32).astype(dtype).astype(np.float64)
    return np.moveaxis((codes * scale).reshape(v.shape), -1, axis)


WIDE = False


def mx_kscale(k):
    if not WIDE:
        return np.ones(k)
    levels = np.array([30, -30])
    if k % 512:
        return np.exp2(np.random.permutation(np.resize(levels, k // 32))).repeat(32)
    a = np.empty((k // 512, 16))
    for p in range(k // 512):
        a[p, :8] = np.random.permutation(np.resize(levels, 8))
        for g in range(8):
            far = levels[np.abs(levels - a[p, g]) >= 10]
            a[p, g + 8] = far[np.random.randint(len(far))]
    return np.exp2(a.ravel()).repeat(32)


BF16 = ml_dtypes.bfloat16


def bf(x):
    return np.asarray(x, np.float32).astype(BF16)


def f64(x):
    return np.asarray(x).astype(np.float64)


B, T, DIM, DQ, H = 1, 512, 2048, 2048, 16
HD = DQ // H
HP = HD // 2
EPS = 1e-6


def rmsnorm(t, g):
    return g * (t * (1.0 / np.sqrt(np.mean(t * t, axis=-1, keepdims=True) + EPS)))


def rope(t, ang):
    b, n, h, d = t.shape
    tp = t.reshape(b, n, h, d // 2, 2)
    cos = np.cos(ang)[None, :, None, :]
    sin = np.sin(ang)[None, :, None, :]
    x0, x1 = tp[..., 0], tp[..., 1]
    return np.stack([x0 * cos - x1 * sin, x0 * sin + x1 * cos], axis=-1).reshape(b, n, h, d)


def setup_inputs():
    s = mx_kscale(DIM)
    w = 1.0 / np.sqrt(DIM)
    return {"x": bf(np.random.standard_normal((B, T, DIM)) * s),
            "freqs": bf(np.random.uniform(-np.pi, np.pi, (T, HP))),
            "Wq": bf(np.random.standard_normal((DIM, DQ)) * w / s[:, None]),
            "bq": bf(np.random.standard_normal(DQ) * 0.3),
            "Wk": bf(np.random.standard_normal((DIM, DQ)) * w / s[:, None]),
            "bk": bf(np.random.standard_normal(DQ) * 0.3),
            "gq": bf(1.0 + 0.1 * np.random.standard_normal(DQ)),
            "gk": bf(1.0 + 0.1 * np.random.standard_normal(DQ))}


def reference(x, freqs, Wq, bq, Wk, bk, gq, gk):
    xq = mxq(f64(x), 2, "e5m2")
    q = rmsnorm((xq @ mxq(f64(Wq), 0, "e5m2")) + f64(bq), f64(gq))
    k = rmsnorm((xq @ mxq(f64(Wk), 0, "e5m2")) + f64(bk), f64(gk))
    ang = f64(freqs)
    return rope(q.reshape(B, T, H, HD), ang), rope(k.reshape(B, T, H, HD), ang)

@@ -1,0 +1,255 @@
+from contextlib import ExitStack
+
+import concourse.mybir as mybir
+from concourse.masks import make_identity
+
+F32 = mybir.dt.float32
+BF16 = mybir.dt.bfloat16
+U32 = mybir.dt.uint32
+U8 = mybir.dt.uint8
+E5X4 = mybir.dt.float8_e5m2_x4
+ACT = mybir.ActivationFunctionType
+ALU = mybir.AluOpType
+AX = mybir.AxisListType
+
+P = 128
+TOK = 512
+DIM = 2048
+DQ = 2048
+HP = 64
+EPS = 1e-6
+HALF_PI = 1.5707963267948966
+K_PASS = 512
+PASSES = DIM // K_PASS
+TT = TOK // P
+CHUNK = 512
+NCHUNK = DQ // CHUNK
+MT = CHUNK // P
+NG = 2 * NCHUNK
+
+V_COLS = (256, 336)
+
+FLOPS = 2 * TOK * DIM * 2 * DQ
+
+
+def tile_causalselfattention_pa_kernel(tc, x, freqs, Wq, bq, Wk, bk, gq, gk, out_0, out_1):
+    nc = tc.nc
+    weights = (Wq, Wk)
+    outs = (out_0.rearrange("b t h d -> (b t) (h d)"), out_1.rearrange("b t h d -> (b t) (h d)"))
+
+    with ExitStack() as ctx:
+        const = ctx.enter_context(tc.tile_pool(name="const", bufs=1))
+        setup = ctx.enter_context(tc.tile_pool(name="setup", bufs=1))
+        wpool = ctx.enter_context(tc.tile_pool(name="wpool", bufs=2))
+        work = ctx.enter_context(tc.tile_pool(name="work", bufs=2))
+        psum = ctx.enter_context(tc.psum_pool(name="psum", bufs=2))
+
+        raw_tiles = {}
+        wg_tiles = {}
+        code_tiles = {}
+        a_tiles = {}
+        p_tiles = {}
+
+        def load_unit(g, c):
+            raw = wpool.tile([P, 4, CHUNK], BF16, name="raw", tag="raw", bufs=8)
+            w = weights[g // NCHUNK]
+            n0 = (g % NCHUNK) * CHUNK
+            nc.sync.dma_start(
+                out=raw[:],
+                in_=w[c * K_PASS : (c + 1) * K_PASS, n0 : n0 + CHUNK].rearrange("(p j) w -> p j w", j=4),
+            )
+            raw_tiles[(g, c)] = raw
+
+        def copy_unit(g, c):
+            raw = raw_tiles[(g, c)]
+            wg = wpool.tile([P, CHUNK, 4], BF16, name="wg", tag="wg", bufs=3, align_bytes=64)
+            src = raw[:].rearrange("p j w -> p w j")
+            vc = V_COLS[0] if g <= NCHUNK else V_COLS[1]
+            nc.vector.tensor_copy(out=wg[:, 0:vc, :], in_=src[:, 0:vc, :])
+            nc.scalar.copy(out=wg[:, vc:CHUNK, :], in_=src[:, vc:CHUNK, :])
+            wg_tiles[(g, c)] = wg
+
+        def quant_unit(g, c):
+            wg = wg_tiles[(g, c)]
+            codes = wpool.tile([P, CHUNK], U32, name="wcodes", tag="wcodes", bufs=8, align_bytes=64)
+            scales = wpool.tile([P, CHUNK], U8, name="wscales", tag="wscales", bufs=8, align_bytes=64)
+            nc.vector.quantize_mx(
+                out=codes[:].bitcast(E5X4), scales=scales[:], in_=wg[:].rearrange("p w j -> p (w j)")
+            )
+            code_tiles[(g, c)] = (codes, scales)
+
+        load_unit(0, 0)
+        load_unit(0, 1)
+        xraw = setup.tile([P, TT, DIM], BF16, name="xraw")
+        xv = x.rearrange("b (t p) k -> p (b t) k", p=P)
+        for t in range(TT):
+            nc.sync.dma_start(out=xraw[:, t, :], in_=xv[:, t, :])
+        load_unit(0, 2)
+        load_unit(0, 3)
+        for c in range(PASSES):
+            load_unit(1, c)
+
+        ident = const.tile([P, P], F32, name="ident")
+        make_identity(nc, ident[:])
+        swap = const.tile([P, P], F32, name="swap")
+        idv = ident[:].rearrange("p (j e) -> p j e", e=2)
+        swv = swap[:].rearrange("p (j e) -> p j e", e=2)
+        nc.vector.tensor_copy(out=swv[:, :, 0:1], in_=idv[:, :, 1:2])
+        nc.vector.tensor_copy(out=swv[:, :, 1:2], in_=idv[:, :, 0:1])
+
+        prm_raw = setup.tile([P, P], BF16, name="prm_raw")
+        nc.vector.memset(prm_raw[:], 0.0)
+        for v, vec in enumerate((bq, bk, gq, gk)):
+            nc.scalar.dma_start(out=prm_raw[16 * v : 16 * v + 16, :], in_=vec.rearrange("(m p) -> m p", p=P))
+        fr_raw = setup.tile([P, TT, HP], BF16, name="fr_raw")
+        nc.scalar.dma_start(out=fr_raw[:], in_=freqs.rearrange("(t p) j -> p t j", p=P))
+        prm_f = setup.tile([P, P], F32, name="prm_f")
+        nc.vector.tensor_copy(out=prm_f[:], in_=prm_raw[:])
+        prm_ps = psum.tile([P, 4 * P], F32, name="prm_ps", tag="ta", bufs=2)
+        nc.tensor.transpose(prm_ps[:, 0:P], prm_f[:], ident[:])
+        prm = const.tile([P, P], F32, name="prm")
+        nc.vector.tensor_copy(out=prm[:], in_=prm_ps[:, 0:P])
+
+        ang = setup.tile([P, TT, HP, 2], F32, name="ang")
+        nc.vector.tensor_copy(out=ang[:, :, :, 0], in_=fr_raw[:])
+        nc.vector.tensor_scalar(out=ang[:, :, :, 1], in0=fr_raw[:], scalar1=-1.0, scalar2=None, op0=ALU.mult)
+        angf = ang[:].rearrange("p t j e -> p (t j e)")
+        sin_tok = setup.tile([P, TT * P], F32, name="sin_tok")
+        nc.scalar.activation(out=sin_tok[:], in_=angf, func=ACT.Sin)
+        absang = setup.tile([P, TT * P], F32, name="absang")
+        nc.scalar.activation(out=absang[:], in_=angf, func=ACT.Abs)
+        cosarg = setup.tile([P, TT * P], F32, name="cosarg")
+        nc.vector.tensor_scalar(
+            out=cosarg[:], in0=absang[:], scalar1=-1.0, scalar2=HALF_PI, op0=ALU.mult, op1=ALU.add
+        )
+        cos_tok = setup.tile([P, TT * P], F32, name="cos_tok")
+        nc.scalar.activation(out=cos_tok[:], in_=cosarg[:], func=ACT.Sin)
+        tables = const.tile([P, 2, TOK], F32, name="tables")
+        for i, tok_major in enumerate((cos_tok, sin_tok)):
+            tb_ps = psum.tile([P, TOK], F32, name="tb_ps", tag="ta", bufs=2)
+            for t in range(TT):
+                nc.tensor.transpose(tb_ps[:, t * P : (t + 1) * P], tok_major[:, t * P : (t + 1) * P], ident[:])
+            nc.vector.tensor_copy(out=tables[:, i, :], in_=tb_ps[:])
+        warm_in = setup.tile([P, 1], F32, name="warm_in")
+        nc.vector.tensor_scalar(out=warm_in[:], in0=cos_tok[:, 0:1], scalar1=0.0, scalar2=1.0, op0=ALU.mult, op1=ALU.add)
+        warm_out = setup.tile([P, 1], F32, name="warm_out")
+        nc.scalar.activation(out=warm_out[:], in_=warm_in[:], func=ACT.Sqrt)
+
+        xcodes = const.tile([P, PASSES, TOK], U32, name="xcodes", align_bytes=64)
+        xscales = const.tile([P, PASSES, TOK], U8, name="xscales", align_bytes=64)
+        xw = xraw[:].bitcast(F32)
+        copy_unit(0, 0)
+        copy_unit(0, 1)
+        quant_unit(0, 0)
+        for c in range(PASSES):
+            xg = setup.tile([P, TOK * 4], BF16, name="xg", tag="xg", bufs=2, align_bytes=64)
+            xgw = xg[:].bitcast(F32)
+            for h in range(2):
+                xt = psum.tile([P, 2, 2, P], F32, name="xt", tag="to", bufs=3)
+                for a in range(2):
+                    for u in range(2):
+                        nc.tensor.transpose(
+                            xt[:, a, u, :], xw[:, 2 * h + a, 256 * c + u : 256 * (c + 1) : 2], ident[:]
+                        )
+                dst = xgw[:, 512 * h : 512 * (h + 1)].rearrange("p (a r u) -> p a r u", a=2, u=2)
+                if h == 0:
+                    nc.vector.tensor_copy(out=dst, in_=xt[:].rearrange("p a u r -> p a r u"))
+                else:
+                    nc.scalar.copy(out=dst, in_=xt[:].rearrange("p a u r -> p a r u"))
+            nc.vector.quantize_mx(out=xcodes[:, c, :].bitcast(E5X4), scales=xscales[:, c, :], in_=xg[:])
+        quant_unit(0, 1)
+        copy_unit(0, 2)
+        copy_unit(0, 3)
+        quant_unit(0, 2)
+        quant_unit(0, 3)
+
+        ssp = const.tile([P, 2, TT, NCHUNK], F32, name="ssp")
+        rstd = const.tile([P, 2, TT], F32, name="rstd")
+
+        def mx_tile(g, m):
+            acc = psum.tile([P, TOK], F32, name="acc", tag="mx", bufs=3)
+            for c in range(PASSES):
+                codes, scales = code_tiles[(g, c)]
+                nc.tensor.matmul_mx(
+                    out=acc[:],
+                    lhsT=codes[:, m * P : (m + 1) * P].bitcast(E5X4),
+                    lhsT_scale=scales[:, m * P : (m + 1) * P],
+                    rhs=xcodes[:, c, :].bitcast(E5X4),
+                    rhs_scale=xscales[:, c, :],
+                    start=(c == 0),
+                    stop=(c == PASSES - 1),
+                )
+            col = 16 * (g // NCHUNK) + (g % NCHUNK) * MT + m
+            a = work.tile([P, TOK], F32, name="a", tag="a", bufs=8)
+            nc.scalar.activation(out=a[:], in_=acc[:], func=ACT.Identity, bias=prm[:, col : col + 1], scale=1.0)
+            a_tiles[(g, m)] = a
+
+        def rope_tile(g, m):
+            col = 32 + 16 * (g // NCHUNK) + (g % NCHUNK) * MT + m
+            a = a_tiles[(g, m)]
+            pr = work.tile([P, 2, TOK], F32, name="pr", tag="pr", bufs=20)
+            nc.vector.scalar_tensor_tensor(
+                out=pr[:], in0=a[:].unsqueeze(1).to_broadcast([P, 2, TOK]), scalar=prm[:, col : col + 1],
+                in1=tables[:], op0=ALU.mult, op1=ALU.mult,
+            )
+            p_tiles[(g, m)] = pr
+
+        def sumsq(g, t):
+            ta = psum.tile([P, CHUNK], F32, name="ta", tag="ta", bufs=2)
+            for m in range(MT):
+                nc.tensor.transpose(ta[:, m * P : (m + 1) * P], a_tiles[(g, m)][:, t * P : (t + 1) * P], ident[:])
+            junk = work.tile([P, CHUNK], F32, name="junk", tag="junk", bufs=2)
+            nc.scalar.activation(
+                out=junk[:], in_=ta[:], func=ACT.Square,
+                accum_out=ssp[:, g // NCHUNK, t, g % NCHUNK : g % NCHUNK + 1],
+            )
+
+        def norm(mat):
+            ss = work.tile([P, TT], F32, name="ss", tag="ss", bufs=2)
+            nc.vector.tensor_reduce(out=ss[:], in_=ssp[:, mat, :, :], axis=AX.X, op=ALU.add)
+            ms = work.tile([P, TT], F32, name="ms", tag="ms", bufs=2)
+            nc.vector.tensor_scalar(out=ms[:], in0=ss[:], scalar1=1.0 / DQ, scalar2=EPS, op0=ALU.mult, op1=ALU.add)
+            sd = work.tile([P, TT], F32, name="sd", tag="sd", bufs=2)
+            nc.scalar.activation(out=sd[:], in_=ms[:], func=ACT.Sqrt)
+            nc.vector.reciprocal(out=rstd[:, mat, :], in_=sd[:])
+
+        def finish(g, t, on_vector, queue, tag, bufs):
+            mat = g // NCHUNK
+            to = psum.tile([P, CHUNK], F32, name="to", tag=tag, bufs=bufs)
+            for m in range(MT):
+                pr = p_tiles[(g, m)]
+                dst = to[:, m * P : (m + 1) * P]
+                nc.tensor.matmul(dst, lhsT=pr[:, 0, t * P : (t + 1) * P], rhs=ident[:], is_transpose=True, start=True, stop=False)
+                nc.tensor.matmul(dst, lhsT=pr[:, 1, t * P : (t + 1) * P], rhs=swap[:], is_transpose=True, start=False, stop=True)
+            st = work.tile([P, CHUNK], F32, name="st", tag="st", bufs=4)
+            if on_vector:
+                nc.vector.tensor_scalar(out=st[:], in0=to[:], scalar1=rstd[:, mat, t : t + 1], scalar2=None, op0=ALU.mult)
+            else:
+                nc.scalar.activation(out=st[:], in_=to[:], func=ACT.Copy, scale=rstd[:, mat, t : t + 1])
+            n0 = (g % NCHUNK) * CHUNK
+            queue.dma_start(out=outs[mat][t * P : (t + 1) * P, n0 : n0 + CHUNK], in_=st[:])
+
+        for g in range(NG):
+            for c in range(PASSES):
+                if g + 2 < NG:
+                    load_unit(g + 2, c)
+            for m in range(MT):
+                if g + 1 < NG:
+                    copy_unit(g + 1, m)
+                    if m > 0:
+                        quant_unit(g + 1, m - 1)
+                mx_tile(g, m)
+                rope_tile(g, m)
+                if g >= NCHUNK:
+                    finish(g - NCHUNK, m, False, nc.gpsimd, "to", 3)
+            if g + 1 < NG:
+                quant_unit(g + 1, MT - 1)
+            for t in range(TT):
+                sumsq(g, t)
+            if g == NCHUNK - 1:
+                norm(0)
+        norm(1)
+        for g in range(NCHUNK, NG):
+            for t in range(TT):
+                tag, bufs = (("to", 3), ("mx", 3), ("ta", 2))[(g * TT + t) % 3]
+                finish(g, t, t % 2 == 1, nc.sync, tag, bufs)

@@ -26,10 +26,27 @@ CHUNK = 512
 NCHUNK = DQ // CHUNK
 MT = CHUNK // P
 NG = 2 * NCHUNK
-
-V_COLS = (256, 336)
+NUNIT = NG * PASSES
+NTILE = NG * MT
+NROUND = NTILE // 2
 
 FLOPS = 2 * TOK * DIM * 2 * DQ
+
+def v_cols(r):
+    if r < 0:
+        return VC[0]
+    if r < 6:
+        return VC[1]
+    return VC[2]
+
+VC = (256, 216, 360)
+PR_BUFS = 20
+ST_BUFS = 6
+FQ = {10: 2, 11: 2, 12: 2, 13: 3, 14: 3, 15: 3}
+RK = {9: 0, 10: 0, 11: 0, 12: 1, 13: 3, 14: 4, 15: 4}
+TAIL_R = 6
+DEPTH = 4
+TAIL_FV = 2
 
 
 def tile_causalselfattention_pa_kernel(tc, x, freqs, Wq, bq, Wk, bk, gq, gk, out_0, out_1):
@@ -38,6 +55,7 @@ def tile_causalselfattention_pa_kernel(tc, x, freqs, Wq, bq, Wk, bk, gq, gk, out
     outs = (out_0.rearrange("b t h d -> (b t) (h d)"), out_1.rearrange("b t h d -> (b t) (h d)"))
 
     with ExitStack() as ctx:
+        ctx.enter_context(tc.manual_schedule())
         const = ctx.enter_context(tc.tile_pool(name="const", bufs=1))
         setup = ctx.enter_context(tc.tile_pool(name="setup", bufs=1))
         wpool = ctx.enter_context(tc.tile_pool(name="wpool", bufs=2))
@@ -49,45 +67,49 @@ def tile_causalselfattention_pa_kernel(tc, x, freqs, Wq, bq, Wk, bk, gq, gk, out
         code_tiles = {}
         a_tiles = {}
         p_tiles = {}
+        ta_tiles = {}
+        to_tiles = {}
 
-        def load_unit(g, c):
+        def load_unit(u):
+            g, c = u // PASSES, u % PASSES
             raw = wpool.tile([P, 4, CHUNK], BF16, name="raw", tag="raw", bufs=8)
-            w = weights[g // NCHUNK]
             n0 = (g % NCHUNK) * CHUNK
             nc.sync.dma_start(
                 out=raw[:],
-                in_=w[c * K_PASS : (c + 1) * K_PASS, n0 : n0 + CHUNK].rearrange("(p j) w -> p j w", j=4),
+                in_=weights[g // NCHUNK][c * K_PASS : (c + 1) * K_PASS, n0 : n0 + CHUNK].rearrange(
+                    "(p j) w -> p j w", j=4
+                ),
             )
-            raw_tiles[(g, c)] = raw
+            raw_tiles[u] = raw
 
-        def copy_unit(g, c):
-            raw = raw_tiles[(g, c)]
-            wg = wpool.tile([P, CHUNK, 4], BF16, name="wg", tag="wg", bufs=3, align_bytes=64)
-            src = raw[:].rearrange("p j w -> p w j")
-            vc = V_COLS[0] if g <= NCHUNK else V_COLS[1]
+        def copy_unit(u, vc):
+            wg = wpool.tile([P, CHUNK, 4], BF16, name="wg", tag="wg", bufs=4, align_bytes=64)
+            src = raw_tiles[u][:].rearrange("p j w -> p w j")
             nc.vector.tensor_copy(out=wg[:, 0:vc, :], in_=src[:, 0:vc, :])
             nc.scalar.copy(out=wg[:, vc:CHUNK, :], in_=src[:, vc:CHUNK, :])
-            wg_tiles[(g, c)] = wg
+            wg_tiles[u] = wg
 
-        def quant_unit(g, c):
-            wg = wg_tiles[(g, c)]
+        def quant_unit(u):
             codes = wpool.tile([P, CHUNK], U32, name="wcodes", tag="wcodes", bufs=8, align_bytes=64)
             scales = wpool.tile([P, CHUNK], U8, name="wscales", tag="wscales", bufs=8, align_bytes=64)
             nc.vector.quantize_mx(
-                out=codes[:].bitcast(E5X4), scales=scales[:], in_=wg[:].rearrange("p w j -> p (w j)")
+                out=codes[:].bitcast(E5X4), scales=scales[:], in_=wg_tiles[u][:].rearrange("p w j -> p (w j)")
             )
-            code_tiles[(g, c)] = (codes, scales)
+            code_tiles[u] = (codes, scales)
 
-        load_unit(0, 0)
-        load_unit(0, 1)
-        xraw = setup.tile([P, TT, DIM], BF16, name="xraw")
+        prm_raw = setup.tile([P, P], BF16, name="prm_raw")
+        nc.vector.memset(prm_raw[:], 0.0)
+        fr_raw = setup.tile([P, TT, HP], BF16, name="fr_raw")
+        nc.scalar.dma_start(out=fr_raw[:], in_=freqs.rearrange("(t p) j -> p t j", p=P))
+        for v, vec in enumerate((bq, bk, gq, gk)):
+            nc.scalar.dma_start(out=prm_raw[16 * v : 16 * v + 16, :], in_=vec.rearrange("(m p) -> m p", p=P))
         xv = x.rearrange("b (t p) k -> p (b t) k", p=P)
-        for t in range(TT):
-            nc.sync.dma_start(out=xraw[:, t, :], in_=xv[:, t, :])
-        load_unit(0, 2)
-        load_unit(0, 3)
+        xraw = []
         for c in range(PASSES):
-            load_unit(1, c)
+            load_unit(c)
+            xr = wpool.tile([P, TT, K_PASS], BF16, name="xraw", tag="raw", bufs=8)
+            nc.sync.dma_start(out=xr[:], in_=xv[:, :, c * K_PASS : (c + 1) * K_PASS])
+            xraw.append(xr)
 
         ident = const.tile([P, P], F32, name="ident")
         make_identity(nc, ident[:])
@@ -97,79 +119,113 @@ def tile_causalselfattention_pa_kernel(tc, x, freqs, Wq, bq, Wk, bk, gq, gk, out
         nc.vector.tensor_copy(out=swv[:, :, 0:1], in_=idv[:, :, 1:2])
         nc.vector.tensor_copy(out=swv[:, :, 1:2], in_=idv[:, :, 0:1])
 
-        prm_raw = setup.tile([P, P], BF16, name="prm_raw")
-        nc.vector.memset(prm_raw[:], 0.0)
-        for v, vec in enumerate((bq, bk, gq, gk)):
-            nc.scalar.dma_start(out=prm_raw[16 * v : 16 * v + 16, :], in_=vec.rearrange("(m p) -> m p", p=P))
-        fr_raw = setup.tile([P, TT, HP], BF16, name="fr_raw")
-        nc.scalar.dma_start(out=fr_raw[:], in_=freqs.rearrange("(t p) j -> p t j", p=P))
-        prm_f = setup.tile([P, P], F32, name="prm_f")
-        nc.vector.tensor_copy(out=prm_f[:], in_=prm_raw[:])
-        prm_ps = psum.tile([P, 4 * P], F32, name="prm_ps", tag="ta", bufs=2)
-        nc.tensor.transpose(prm_ps[:, 0:P], prm_f[:], ident[:])
-        prm = const.tile([P, P], F32, name="prm")
-        nc.vector.tensor_copy(out=prm[:], in_=prm_ps[:, 0:P])
-
         ang = setup.tile([P, TT, HP, 2], F32, name="ang")
         nc.vector.tensor_copy(out=ang[:, :, :, 0], in_=fr_raw[:])
         nc.vector.tensor_scalar(out=ang[:, :, :, 1], in0=fr_raw[:], scalar1=-1.0, scalar2=None, op0=ALU.mult)
         angf = ang[:].rearrange("p t j e -> p (t j e)")
-        sin_tok = setup.tile([P, TT * P], F32, name="sin_tok")
-        nc.scalar.activation(out=sin_tok[:], in_=angf, func=ACT.Sin)
         absang = setup.tile([P, TT * P], F32, name="absang")
         nc.scalar.activation(out=absang[:], in_=angf, func=ACT.Abs)
+        sin_tok = setup.tile([P, TT * P], F32, name="sin_tok")
+        nc.scalar.activation(out=sin_tok[:], in_=angf, func=ACT.Sin)
         cosarg = setup.tile([P, TT * P], F32, name="cosarg")
         nc.vector.tensor_scalar(
             out=cosarg[:], in0=absang[:], scalar1=-1.0, scalar2=HALF_PI, op0=ALU.mult, op1=ALU.add
         )
         cos_tok = setup.tile([P, TT * P], F32, name="cos_tok")
         nc.scalar.activation(out=cos_tok[:], in_=cosarg[:], func=ACT.Sin)
-        tables = const.tile([P, 2, TOK], F32, name="tables")
-        for i, tok_major in enumerate((cos_tok, sin_tok)):
-            tb_ps = psum.tile([P, TOK], F32, name="tb_ps", tag="ta", bufs=2)
-            for t in range(TT):
-                nc.tensor.transpose(tb_ps[:, t * P : (t + 1) * P], tok_major[:, t * P : (t + 1) * P], ident[:])
-            nc.vector.tensor_copy(out=tables[:, i, :], in_=tb_ps[:])
+        prm_f = setup.tile([P, P], F32, name="prm_f")
+        nc.vector.tensor_copy(out=prm_f[:], in_=prm_raw[:])
         warm_in = setup.tile([P, 1], F32, name="warm_in")
-        nc.vector.tensor_scalar(out=warm_in[:], in0=cos_tok[:, 0:1], scalar1=0.0, scalar2=1.0, op0=ALU.mult, op1=ALU.add)
+        nc.vector.memset(warm_in[:], 1.0)
         warm_out = setup.tile([P, 1], F32, name="warm_out")
         nc.scalar.activation(out=warm_out[:], in_=warm_in[:], func=ACT.Sqrt)
 
+        copy_unit(0, v_cols(-1))
+
+        prm_ps = psum.tile([P, 4 * P], F32, name="prm_ps", tag="mx", bufs=3)
+        nc.tensor.transpose(prm_ps[:, 0:P], prm_f[:], ident[:])
+        tables = const.tile([P, 2, TOK], F32, name="tables")
+        tb_ps = []
+        for i, tok_major in enumerate((cos_tok, sin_tok)):
+            tb = psum.tile([P, TOK], F32, name="tb_ps", tag="mx", bufs=3)
+            for t in range(TT):
+                nc.tensor.transpose(tb[:, t * P : (t + 1) * P], tok_major[:, t * P : (t + 1) * P], ident[:])
+            tb_ps.append(tb)
+
         xcodes = const.tile([P, PASSES, TOK], U32, name="xcodes", align_bytes=64)
         xscales = const.tile([P, PASSES, TOK], U8, name="xscales", align_bytes=64)
-        xw = xraw[:].bitcast(F32)
-        copy_unit(0, 0)
-        copy_unit(0, 1)
-        quant_unit(0, 0)
-        for c in range(PASSES):
-            xg = setup.tile([P, TOK * 4], BF16, name="xg", tag="xg", bufs=2, align_bytes=64)
-            xgw = xg[:].bitcast(F32)
+        xt_tiles = {}
+        xg_tiles = {}
+
+        def x_transposes(c):
+            xw = xraw[c][:].bitcast(F32)
             for h in range(2):
-                xt = psum.tile([P, 2, 2, P], F32, name="xt", tag="to", bufs=3)
+                tag, bufs = (("to", 3), ("ta", 2))[h]
+                xt = psum.tile([P, 2, 2, P], F32, name="xt", tag=tag, bufs=bufs)
                 for a in range(2):
                     for u in range(2):
-                        nc.tensor.transpose(
-                            xt[:, a, u, :], xw[:, 2 * h + a, 256 * c + u : 256 * (c + 1) : 2], ident[:]
-                        )
+                        nc.tensor.transpose(xt[:, a, u, :], xw[:, 2 * h + a, u : 256 : 2], ident[:])
+                xt_tiles[(c, h)] = xt
+
+        def x_copies(c):
+            xg = wpool.tile([P, TOK * 4], BF16, name="xg", tag="wg", bufs=4, align_bytes=64)
+            xgw = xg[:].bitcast(F32)
+            for h in range(2):
                 dst = xgw[:, 512 * h : 512 * (h + 1)].rearrange("p (a r u) -> p a r u", a=2, u=2)
+                src = xt_tiles[(c, h)][:].rearrange("p a u r -> p a r u")
                 if h == 0:
-                    nc.vector.tensor_copy(out=dst, in_=xt[:].rearrange("p a u r -> p a r u"))
+                    nc.vector.tensor_copy(out=dst, in_=src)
                 else:
-                    nc.scalar.copy(out=dst, in_=xt[:].rearrange("p a u r -> p a r u"))
-            nc.vector.quantize_mx(out=xcodes[:, c, :].bitcast(E5X4), scales=xscales[:, c, :], in_=xg[:])
-        quant_unit(0, 1)
-        copy_unit(0, 2)
-        copy_unit(0, 3)
-        quant_unit(0, 2)
-        quant_unit(0, 3)
+                    nc.scalar.copy(out=dst, in_=src)
+            xg_tiles[c] = xg
+
+        def x_quant(c):
+            nc.vector.quantize_mx(out=xcodes[:, c, :].bitcast(E5X4), scales=xscales[:, c, :], in_=xg_tiles[c][:])
+
+        prm = const.tile([P, P], F32, name="prm")
+        x_transposes(0)
+        nc.vector.tensor_copy(out=prm[:], in_=prm_ps[:, 0:P])
+        nc.vector.tensor_copy(out=tables[:, 0, :], in_=tb_ps[0][:])
+        nc.scalar.copy(out=tables[:, 1, :], in_=tb_ps[1][:])
+        load_unit(4)
+        x_copies(0)
+        load_unit(5)
+        copy_unit(1, v_cols(-1))
+        load_unit(6)
+        x_transposes(1)
+        x_quant(0)
+        quant_unit(0)
+        x_copies(1)
+        load_unit(7)
+        copy_unit(2, v_cols(-1))
+        load_unit(8)
+        x_transposes(2)
+        x_quant(1)
+        quant_unit(1)
+        x_copies(2)
+        load_unit(9)
+        copy_unit(3, v_cols(-1))
+        load_unit(10)
+        x_transposes(3)
+        x_quant(2)
+        quant_unit(2)
+        x_copies(3)
+        load_unit(11)
+        copy_unit(4, v_cols(-1))
+        load_unit(12)
+        x_quant(3)
+        quant_unit(3)
+        copy_unit(5, v_cols(-1))
+        load_unit(13)
 
         ssp = const.tile([P, 2, TT, NCHUNK], F32, name="ssp")
         rstd = const.tile([P, 2, TT], F32, name="rstd")
 
-        def mx_tile(g, m):
+        def mx_tile(s):
+            g, m = s // MT, s % MT
             acc = psum.tile([P, TOK], F32, name="acc", tag="mx", bufs=3)
             for c in range(PASSES):
-                codes, scales = code_tiles[(g, c)]
+                codes, scales = code_tiles[g * PASSES + c]
                 nc.tensor.matmul_mx(
                     out=acc[:],
                     lhsT=codes[:, m * P : (m + 1) * P].bitcast(E5X4),
@@ -179,77 +235,154 @@ def tile_causalselfattention_pa_kernel(tc, x, freqs, Wq, bq, Wk, bk, gq, gk, out
                     start=(c == 0),
                     stop=(c == PASSES - 1),
                 )
-            col = 16 * (g // NCHUNK) + (g % NCHUNK) * MT + m
-            a = work.tile([P, TOK], F32, name="a", tag="a", bufs=8)
-            nc.scalar.activation(out=a[:], in_=acc[:], func=ACT.Identity, bias=prm[:, col : col + 1], scale=1.0)
-            a_tiles[(g, m)] = a
+            return acc
 
-        def rope_tile(g, m):
-            col = 32 + 16 * (g // NCHUNK) + (g % NCHUNK) * MT + m
-            a = a_tiles[(g, m)]
-            pr = work.tile([P, 2, TOK], F32, name="pr", tag="pr", bufs=20)
+        def bias_tile(s, acc):
+            a = work.tile([P, TOK], F32, name="a", tag="a", bufs=16)
+            nc.scalar.activation(out=a[:], in_=acc[:], func=ACT.Identity, bias=prm[:, s : s + 1], scale=1.0)
+            a_tiles[s] = a
+
+        def rope_tile(s):
+            pr = work.tile([P, 2, TOK], F32, name="pr", tag="pr", bufs=PR_BUFS)
             nc.vector.scalar_tensor_tensor(
-                out=pr[:], in0=a[:].unsqueeze(1).to_broadcast([P, 2, TOK]), scalar=prm[:, col : col + 1],
-                in1=tables[:], op0=ALU.mult, op1=ALU.mult,
+                out=pr[:], in0=a_tiles[s][:].unsqueeze(1).to_broadcast([P, 2, TOK]),
+                scalar=prm[:, 32 + s : 33 + s], in1=tables[:], op0=ALU.mult, op1=ALU.mult,
             )
-            p_tiles[(g, m)] = pr
+            p_tiles[s] = pr
 
-        def sumsq(g, t):
-            ta = psum.tile([P, CHUNK], F32, name="ta", tag="ta", bufs=2)
+        def sq_transposes(g, t, tag, bufs):
+            ta = psum.tile([P, CHUNK], F32, name="ta", tag=tag, bufs=bufs)
             for m in range(MT):
-                nc.tensor.transpose(ta[:, m * P : (m + 1) * P], a_tiles[(g, m)][:, t * P : (t + 1) * P], ident[:])
+                nc.tensor.transpose(ta[:, m * P : (m + 1) * P], a_tiles[g * MT + m][:, t * P : (t + 1) * P], ident[:])
+            ta_tiles[(g, t)] = ta
+
+        def sq_sum(g, t):
             junk = work.tile([P, CHUNK], F32, name="junk", tag="junk", bufs=2)
             nc.scalar.activation(
-                out=junk[:], in_=ta[:], func=ACT.Square,
+                out=junk[:], in_=ta_tiles[(g, t)][:], func=ACT.Square,
                 accum_out=ssp[:, g // NCHUNK, t, g % NCHUNK : g % NCHUNK + 1],
             )
 
-        def norm(mat):
-            ss = work.tile([P, TT], F32, name="ss", tag="ss", bufs=2)
-            nc.vector.tensor_reduce(out=ss[:], in_=ssp[:, mat, :, :], axis=AX.X, op=ALU.add)
-            ms = work.tile([P, TT], F32, name="ms", tag="ms", bufs=2)
-            nc.vector.tensor_scalar(out=ms[:], in0=ss[:], scalar1=1.0 / DQ, scalar2=EPS, op0=ALU.mult, op1=ALU.add)
-            sd = work.tile([P, TT], F32, name="sd", tag="sd", bufs=2)
-            nc.scalar.activation(out=sd[:], in_=ms[:], func=ACT.Sqrt)
-            nc.vector.reciprocal(out=rstd[:, mat, :], in_=sd[:])
+        stat = const.tile([P, 2, 3, TT], F32, name="stat")
 
-        def finish(g, t, on_vector, queue, tag, bufs):
-            mat = g // NCHUNK
+        def norm_mean(mat):
+            nc.vector.tensor_reduce(out=stat[:, mat, 0, :], in_=ssp[:, mat, :, :], axis=AX.X, op=ALU.add)
+            nc.vector.tensor_scalar(
+                out=stat[:, mat, 1, :], in0=stat[:, mat, 0, :], scalar1=1.0 / DQ, scalar2=EPS, op0=ALU.mult, op1=ALU.add
+            )
+
+        def norm_sqrt(mat):
+            nc.scalar.activation(out=stat[:, mat, 2, :], in_=stat[:, mat, 1, :], func=ACT.Sqrt)
+
+        def norm_recip(mat):
+            nc.vector.reciprocal(out=rstd[:, mat, :], in_=stat[:, mat, 2, :])
+
+        def out_transposes(j, tag, bufs):
+            g, t = j // TT, j % TT
             to = psum.tile([P, CHUNK], F32, name="to", tag=tag, bufs=bufs)
             for m in range(MT):
-                pr = p_tiles[(g, m)]
+                pr = p_tiles[g * MT + m]
                 dst = to[:, m * P : (m + 1) * P]
                 nc.tensor.matmul(dst, lhsT=pr[:, 0, t * P : (t + 1) * P], rhs=ident[:], is_transpose=True, start=True, stop=False)
                 nc.tensor.matmul(dst, lhsT=pr[:, 1, t * P : (t + 1) * P], rhs=swap[:], is_transpose=True, start=False, stop=True)
-            st = work.tile([P, CHUNK], F32, name="st", tag="st", bufs=4)
-            if on_vector:
-                nc.vector.tensor_scalar(out=st[:], in0=to[:], scalar1=rstd[:, mat, t : t + 1], scalar2=None, op0=ALU.mult)
-            else:
-                nc.scalar.activation(out=st[:], in_=to[:], func=ACT.Copy, scale=rstd[:, mat, t : t + 1])
-            n0 = (g % NCHUNK) * CHUNK
-            queue.dma_start(out=outs[mat][t * P : (t + 1) * P, n0 : n0 + CHUNK], in_=st[:])
+            to_tiles[j] = to
 
-        for g in range(NG):
-            for c in range(PASSES):
-                if g + 2 < NG:
-                    load_unit(g + 2, c)
-            for m in range(MT):
-                if g + 1 < NG:
-                    copy_unit(g + 1, m)
-                    if m > 0:
-                        quant_unit(g + 1, m - 1)
-                mx_tile(g, m)
-                rope_tile(g, m)
-                if g >= NCHUNK:
-                    finish(g - NCHUNK, m, False, nc.gpsimd, "to", 3)
-            if g + 1 < NG:
-                quant_unit(g + 1, MT - 1)
-            for t in range(TT):
-                sumsq(g, t)
-            if g == NCHUNK - 1:
-                norm(0)
-        norm(1)
-        for g in range(NCHUNK, NG):
-            for t in range(TT):
-                tag, bufs = (("to", 3), ("mx", 3), ("ta", 2))[(g * TT + t) % 3]
-                finish(g, t, t % 2 == 1, nc.sync, tag, bufs)
+        def out_store(j, on_vector, late=0):
+            g, t = j // TT, j % TT
+            mat = g // NCHUNK
+            if late % 3 == 1:
+                st = wpool.tile([P, CHUNK], F32, name="st", tag="raw", bufs=8)
+            elif late % 3 == 2:
+                st = wpool.tile([P, CHUNK], F32, name="st", tag="wg", bufs=4, align_bytes=64)
+            else:
+                st = work.tile([P, CHUNK], F32, name="st", tag="st", bufs=ST_BUFS)
+            if on_vector:
+                nc.vector.tensor_scalar(out=st[:], in0=to_tiles[j][:], scalar1=rstd[:, mat, t : t + 1], scalar2=None, op0=ALU.mult)
+            else:
+                nc.scalar.activation(out=st[:], in_=to_tiles[j][:], func=ACT.Copy, scale=rstd[:, mat, t : t + 1])
+            n0 = (g % NCHUNK) * CHUNK
+            nc.sync.dma_start(out=outs[mat][t * P : (t + 1) * P, n0 : n0 + CHUNK], in_=st[:])
+
+        pend_sq = []
+        pend_out = []
+        next_fq = 0
+        next_rk = NTILE // 2
+        for r in range(NROUND):
+            acc0 = mx_tile(2 * r)
+            acc1 = mx_tile(2 * r + 1)
+            q_done = bool(pend_sq) and pend_sq[-1] == (NCHUNK - 1, TT - 1)
+            for g, t in pend_sq:
+                sq_sum(g, t)
+            pend_sq = []
+            if q_done:
+                norm_mean(0)
+            for j in pend_out:
+                out_store(j, False)
+            pend_out = []
+            if 1 <= r <= NROUND // 2:
+                rope_tile(2 * r - 2)
+                rope_tile(2 * r - 1)
+            for i in range(RK.get(r, 0)):
+                rope_tile(next_rk)
+                next_rk += 1
+            if 2 * r + 5 < NUNIT:
+                quant_unit(2 * r + 4)
+                quant_unit(2 * r + 5)
+            bias_tile(2 * r, acc0)
+            bias_tile(2 * r + 1, acc1)
+            if q_done:
+                norm_sqrt(0)
+            if r >= 2:
+                g = (r - 2) // 2
+                for t in (2 * (r % 2), 2 * (r % 2) + 1):
+                    sq_transposes(g, t, "ta", 2)
+                    pend_sq.append((g, t))
+            for i in range(FQ.get(r, 0)):
+                out_transposes(next_fq, "to", 3)
+                pend_out.append(next_fq)
+                next_fq += 1
+            if 2 * r + 7 < NUNIT:
+                copy_unit(2 * r + 6, v_cols(r))
+                copy_unit(2 * r + 7, v_cols(r))
+            if q_done:
+                norm_recip(0)
+            if 2 * r + 15 < NUNIT:
+                load_unit(2 * r + 14)
+                load_unit(2 * r + 15)
+
+        for i, t in enumerate(range(TT)):
+            tag, bufs = (("mx", 3), ("mx", 3), ("mx", 3), ("to", 3))[i]
+            sq_transposes(NG - 1, t, tag, bufs)
+        for g, t in pend_sq:
+            sq_sum(g, t)
+        late = 0
+        for j in pend_out:
+            out_store(j, False, late)
+            late += 1
+        for i in range(TAIL_R):
+            if next_rk < NTILE:
+                rope_tile(next_rk)
+                next_rk += 1
+        for t in range(TT):
+            sq_sum(NG - 1, t)
+        norm_mean(1)
+        norm_sqrt(1)
+        norm_recip(1)
+        pend = []
+        k = 0
+        for j in range(next_fq, NG * TT):
+            need = (j // TT) * MT + MT
+            while next_rk < min(need, NTILE):
+                rope_tile(next_rk)
+                next_rk += 1
+            tag, bufs = (("ta", 2), ("to", 3), ("mx", 3))[k % 3]
+            out_transposes(j, tag, bufs)
+            pend.append(j)
+            k += 1
+            if len(pend) > DEPTH:
+                out_store(pend[0], TAIL_FV > 0 and late % TAIL_FV == TAIL_FV - 1, late)
+                late += 1
+                pend = pend[1:]
+        for j in pend:
+            out_store(j, TAIL_FV > 0 and late % TAIL_FV == TAIL_FV - 1, late)
+            late += 1

@@ -84,9 +84,15 @@ def tile_causalselfattention_pa_kernel(tc, x, freqs, Wq, bq, Wk, bk, gq, gk, out
 
         def copy_unit(u, vc):
             wg = wpool.tile([P, CHUNK, 4], BF16, name="wg", tag="wg", bufs=4, align_bytes=64)
-            src = raw_tiles[u][:].rearrange("p j w -> p w j")
-            nc.vector.tensor_copy(out=wg[:, 0:vc, :], in_=src[:, 0:vc, :])
-            nc.scalar.copy(out=wg[:, vc:CHUNK, :], in_=src[:, vc:CHUNK, :])
+            raw = raw_tiles[u]
+            nc.vector.tensor_copy(
+                out=wg[:, 0:vc, :].rearrange("p (c i) t -> p c t i", i=4),
+                in_=raw[:, :, 0:vc].rearrange("p t (c i) -> p c t i", i=4),
+            )
+            nc.scalar.copy(
+                out=wg[:, vc:CHUNK, :].rearrange("p (c i) t -> p c t i", i=4),
+                in_=raw[:, :, vc:CHUNK].rearrange("p t (c i) -> p c t i", i=4),
+            )
             wg_tiles[u] = wg
 
         def quant_unit(u):

@@ -35,16 +35,19 @@ FLOPS = 2 * TOK * DIM * 2 * DQ
 def v_cols(r):
     if r < 0:
         return VC[0]
-    if r < 6:
+    if r < VT:
         return VC[1]
     return VC[2]
 
 VC = (256, 216, 360)
 PR_BUFS = 20
 ST_BUFS = 6
-FQ = {10: 2, 11: 2, 12: 2, 13: 3, 14: 3, 15: 3}
-RK = {9: 0, 10: 0, 11: 0, 12: 1, 13: 3, 14: 4, 15: 4}
-TAIL_R = 6
+FQ = {10: 2, 11: 2, 12: 3, 13: 3, 14: 3, 15: 3}
+RS = {1: 2, 2: 2, 3: 2, 4: 2, 5: 2, 6: 2, 7: 2, 8: 2, 12: 1, 13: 3, 14: 4, 15: 4}
+A_BUFS = 16
+VT = 6
+TAIL_R = 2
+TAIL_R2 = 0
 DEPTH = 4
 TAIL_FV = 2
 
@@ -244,7 +247,7 @@ def tile_causalselfattention_pa_kernel(tc, x, freqs, Wq, bq, Wk, bk, gq, gk, out
             return acc
 
         def bias_tile(s, acc):
-            a = work.tile([P, TOK], F32, name="a", tag="a", bufs=16)
+            a = work.tile([P, TOK], F32, name="a", tag="a", bufs=A_BUFS)
             nc.scalar.activation(out=a[:], in_=acc[:], func=ACT.Identity, bias=prm[:, s : s + 1], scale=1.0)
             a_tiles[s] = a
 
@@ -312,7 +315,7 @@ def tile_causalselfattention_pa_kernel(tc, x, freqs, Wq, bq, Wk, bk, gq, gk, out
         pend_sq = []
         pend_out = []
         next_fq = 0
-        next_rk = NTILE // 2
+        next_rk = 0
         for r in range(NROUND):
             acc0 = mx_tile(2 * r)
             acc1 = mx_tile(2 * r + 1)
@@ -325,10 +328,8 @@ def tile_causalselfattention_pa_kernel(tc, x, freqs, Wq, bq, Wk, bk, gq, gk, out
             for j in pend_out:
                 out_store(j, False)
             pend_out = []
-            if 1 <= r <= NROUND // 2:
-                rope_tile(2 * r - 2)
-                rope_tile(2 * r - 1)
-            for i in range(RK.get(r, 0)):
+            for i in range(RS.get(r, 0)):
+                assert next_rk < 2 * r
                 rope_tile(next_rk)
                 next_rk += 1
             if 2 * r + 5 < NUNIT:
@@ -344,6 +345,7 @@ def tile_causalselfattention_pa_kernel(tc, x, freqs, Wq, bq, Wk, bk, gq, gk, out
                     sq_transposes(g, t, "ta", 2)
                     pend_sq.append((g, t))
             for i in range(FQ.get(r, 0)):
+                assert (next_fq // TT) * MT + MT <= next_rk
                 out_transposes(next_fq, "to", 3)
                 pend_out.append(next_fq)
                 next_fq += 1
@@ -356,27 +358,41 @@ def tile_causalselfattention_pa_kernel(tc, x, freqs, Wq, bq, Wk, bk, gq, gk, out
                 load_unit(2 * r + 14)
                 load_unit(2 * r + 15)
 
-        for i, t in enumerate(range(TT)):
-            tag, bufs = (("mx", 3), ("mx", 3), ("mx", 3), ("to", 3))[i]
-            sq_transposes(NG - 1, t, tag, bufs)
-        for g, t in pend_sq:
-            sq_sum(g, t)
         late = 0
+        for i, t in enumerate(range(TT)):
+            tag, bufs = (("mx", 3), ("mx", 3), ("mx", 3), ("ta", 2))[i]
+            if i == 3:
+                for g2, t2 in pend_sq:
+                    sq_sum(g2, t2)
+            sq_transposes(NG - 1, t, tag, bufs)
         for j in pend_out:
-            out_store(j, False, late)
+            out_store(j, True, late)
             late += 1
+        rest_q = list(range(next_fq, NCHUNK * TT))
+        while next_rk < NTILE // 2:
+            rope_tile(next_rk)
+            next_rk += 1
+        for i, j in enumerate(rest_q):
+            out_transposes(j, "to", 3)
+        for t in range(TT):
+            sq_sum(NG - 1, t)
         for i in range(TAIL_R):
             if next_rk < NTILE:
                 rope_tile(next_rk)
                 next_rk += 1
-        for t in range(TT):
-            sq_sum(NG - 1, t)
+        for j in rest_q:
+            out_store(j, True, late)
+            late += 1
+        for i in range(TAIL_R2):
+            if next_rk < NTILE:
+                rope_tile(next_rk)
+                next_rk += 1
         norm_mean(1)
         norm_sqrt(1)
         norm_recip(1)
         pend = []
         k = 0
-        for j in range(next_fq, NG * TT):
+        for j in range(NCHUNK * TT, NG * TT):
             need = (j // TT) * MT + MT
             while next_rk < min(need, NTILE):
                 rope_tile(next_rk)

@@ -35,19 +35,16 @@ FLOPS = 2 * TOK * DIM * 2 * DQ
 def v_cols(r):
     if r < 0:
         return VC[0]
-    if r < VT:
+    if r < 6:
         return VC[1]
     return VC[2]
 
 VC = (256, 216, 360)
 PR_BUFS = 20
 ST_BUFS = 6
-FQ = {10: 2, 11: 2, 12: 3, 13: 3, 14: 3, 15: 3}
-RS = {1: 2, 2: 2, 3: 2, 4: 2, 5: 2, 6: 2, 7: 2, 8: 2, 12: 1, 13: 3, 14: 4, 15: 4}
-A_BUFS = 16
-VT = 6
-TAIL_R = 2
-TAIL_R2 = 0
+FQ = {10: 2, 11: 2, 12: 2, 13: 3, 14: 3, 15: 3}
+RK = {9: 0, 10: 0, 11: 0, 12: 1, 13: 3, 14: 4, 15: 4}
+TAIL_R = 6
 DEPTH = 4
 TAIL_FV = 2
 
@@ -58,7 +55,7 @@ def tile_causalselfattention_pa_kernel(tc, x, freqs, Wq, bq, Wk, bk, gq, gk, out
     outs = (out_0.rearrange("b t h d -> (b t) (h d)"), out_1.rearrange("b t h d -> (b t) (h d)"))
 
     with ExitStack() as ctx:
-        ctx.enter_context(tc.manual_schedule())
+        ctx.enter_context(tc.manual_schedule(engines={mybir.EngineType.PE}))
         const = ctx.enter_context(tc.tile_pool(name="const", bufs=1))
         setup = ctx.enter_context(tc.tile_pool(name="setup", bufs=1))
         wpool = ctx.enter_context(tc.tile_pool(name="wpool", bufs=2))
@@ -247,7 +244,7 @@ def tile_causalselfattention_pa_kernel(tc, x, freqs, Wq, bq, Wk, bk, gq, gk, out
             return acc
 
         def bias_tile(s, acc):
-            a = work.tile([P, TOK], F32, name="a", tag="a", bufs=A_BUFS)
+            a = work.tile([P, TOK], F32, name="a", tag="a", bufs=16)
             nc.scalar.activation(out=a[:], in_=acc[:], func=ACT.Identity, bias=prm[:, s : s + 1], scale=1.0)
             a_tiles[s] = a
 
@@ -315,7 +312,7 @@ def tile_causalselfattention_pa_kernel(tc, x, freqs, Wq, bq, Wk, bk, gq, gk, out
         pend_sq = []
         pend_out = []
         next_fq = 0
-        next_rk = 0
+        next_rk = NTILE // 2
         for r in range(NROUND):
             acc0 = mx_tile(2 * r)
             acc1 = mx_tile(2 * r + 1)
@@ -328,8 +325,10 @@ def tile_causalselfattention_pa_kernel(tc, x, freqs, Wq, bq, Wk, bk, gq, gk, out
             for j in pend_out:
                 out_store(j, False)
             pend_out = []
-            for i in range(RS.get(r, 0)):
-                assert next_rk < 2 * r
+            if 1 <= r <= NROUND // 2:
+                rope_tile(2 * r - 2)
+                rope_tile(2 * r - 1)
+            for i in range(RK.get(r, 0)):
                 rope_tile(next_rk)
                 next_rk += 1
             if 2 * r + 5 < NUNIT:
@@ -345,7 +344,6 @@ def tile_causalselfattention_pa_kernel(tc, x, freqs, Wq, bq, Wk, bk, gq, gk, out
                     sq_transposes(g, t, "ta", 2)
                     pend_sq.append((g, t))
             for i in range(FQ.get(r, 0)):
-                assert (next_fq // TT) * MT + MT <= next_rk
                 out_transposes(next_fq, "to", 3)
                 pend_out.append(next_fq)
                 next_fq += 1
@@ -358,41 +356,27 @@ def tile_causalselfattention_pa_kernel(tc, x, freqs, Wq, bq, Wk, bk, gq, gk, out
                 load_unit(2 * r + 14)
                 load_unit(2 * r + 15)
 
-        late = 0
         for i, t in enumerate(range(TT)):
-            tag, bufs = (("mx", 3), ("mx", 3), ("mx", 3), ("ta", 2))[i]
-            if i == 3:
-                for g2, t2 in pend_sq:
-                    sq_sum(g2, t2)
+            tag, bufs = (("mx", 3), ("mx", 3), ("mx", 3), ("to", 3))[i]
             sq_transposes(NG - 1, t, tag, bufs)
+        for g, t in pend_sq:
+            sq_sum(g, t)
+        late = 0
         for j in pend_out:
-            out_store(j, True, late)
+            out_store(j, False, late)
             late += 1
-        rest_q = list(range(next_fq, NCHUNK * TT))
-        while next_rk < NTILE // 2:
-            rope_tile(next_rk)
-            next_rk += 1
-        for i, j in enumerate(rest_q):
-            out_transposes(j, "to", 3)
-        for t in range(TT):
-            sq_sum(NG - 1, t)
         for i in range(TAIL_R):
             if next_rk < NTILE:
                 rope_tile(next_rk)
                 next_rk += 1
-        for j in rest_q:
-            out_store(j, True, late)
-            late += 1
-        for i in range(TAIL_R2):
-            if next_rk < NTILE:
-                rope_tile(next_rk)
-                next_rk += 1
+        for t in range(TT):
+            sq_sum(NG - 1, t)
         norm_mean(1)
         norm_sqrt(1)
         norm_recip(1)
         pend = []
         k = 0
-        for j in range(NCHUNK * TT, NG * TT):
+        for j in range(next_fq, NG * TT):
             need = (j // TT) * MT + MT
             while next_rk < min(need, NTILE):
                 rope_tile(next_rk)

@@ -32,14 +32,19 @@ NROUND = NTILE // 2
 
 FLOPS = 2 * TOK * DIM * 2 * DQ
 
-def v_cols(r):
-    if r < 0:
-        return VC[0]
-    if r < 6:
-        return VC[1]
-    return VC[2]
+def shares(r):
+    if r < -1:
+        return (256, 0)
+    if r < 1:
+        return (216, 0)
+    if r < 5:
+        return (112, GC)
+    if r <= LAST_WINDOW:
+        return (256, GC)
+    return (360, 0)
 
-VC = (256, 216, 360)
+GC = 160
+LAST_WINDOW = 9
 PR_BUFS = 20
 ST_BUFS = 6
 FQ = {10: 2, 11: 2, 12: 2, 13: 3, 14: 3, 15: 3}
@@ -55,7 +60,7 @@ def tile_causalselfattention_pa_kernel(tc, x, freqs, Wq, bq, Wk, bk, gq, gk, out
     outs = (out_0.rearrange("b t h d -> (b t) (h d)"), out_1.rearrange("b t h d -> (b t) (h d)"))
 
     with ExitStack() as ctx:
-        ctx.enter_context(tc.manual_schedule(engines={mybir.EngineType.PE}))
+        ctx.enter_context(tc.manual_schedule(engines={mybir.EngineType.PE, mybir.EngineType.DVE, mybir.EngineType.Pool}))
         const = ctx.enter_context(tc.tile_pool(name="const", bufs=1))
         setup = ctx.enter_context(tc.tile_pool(name="setup", bufs=1))
         wpool = ctx.enter_context(tc.tile_pool(name="wpool", bufs=2))
@@ -82,18 +87,33 @@ def tile_causalselfattention_pa_kernel(tc, x, freqs, Wq, bq, Wk, bk, gq, gk, out
             )
             raw_tiles[u] = raw
 
-        def copy_unit(u, vc):
+        def copy_g(u, sh):
             wg = wpool.tile([P, CHUNK, 4], BF16, name="wg", tag="wg", bufs=4, align_bytes=64)
+            wg_tiles[u] = wg
+            g0 = CHUNK - sh[1]
+            if sh[1] > 0:
+                nc.gpsimd.tensor_scalar(
+                    out=wg[:, g0:CHUNK, :], in0=raw_tiles[u][:, :, g0:CHUNK].rearrange("p t w -> p w t"),
+                    scalar1=1.0, scalar2=0.0, op0=ALU.mult, op1=ALU.add,
+                )
+
+        def copy_vs(u, sh):
+            wg = wg_tiles[u]
             raw = raw_tiles[u]
+            vc = sh[0]
+            g0 = CHUNK - sh[1]
             nc.vector.tensor_copy(
                 out=wg[:, 0:vc, :].rearrange("p (c i) t -> p c t i", i=4),
                 in_=raw[:, :, 0:vc].rearrange("p t (c i) -> p c t i", i=4),
             )
             nc.scalar.copy(
-                out=wg[:, vc:CHUNK, :].rearrange("p (c i) t -> p c t i", i=4),
-                in_=raw[:, :, vc:CHUNK].rearrange("p t (c i) -> p c t i", i=4),
+                out=wg[:, vc:g0, :].rearrange("p (c i) t -> p c t i", i=4),
+                in_=raw[:, :, vc:g0].rearrange("p t (c i) -> p c t i", i=4),
             )
-            wg_tiles[u] = wg
+
+        def copy_unit(u, sh):
+            copy_g(u, sh)
+            copy_vs(u, sh)
 
         def quant_unit(u):
             codes = wpool.tile([P, CHUNK], U32, name="wcodes", tag="wcodes", bufs=8, align_bytes=64)
@@ -146,14 +166,14 @@ def tile_causalselfattention_pa_kernel(tc, x, freqs, Wq, bq, Wk, bk, gq, gk, out
         warm_out = setup.tile([P, 1], F32, name="warm_out")
         nc.scalar.activation(out=warm_out[:], in_=warm_in[:], func=ACT.Sqrt)
 
-        copy_unit(0, v_cols(-1))
+        copy_unit(0, shares(-2))
 
         prm_ps = psum.tile([P, 4 * P], F32, name="prm_ps", tag="mx", bufs=3)
         nc.tensor.transpose(prm_ps[:, 0:P], prm_f[:], ident[:])
         tables = const.tile([P, 2, TOK], F32, name="tables")
         tb_ps = []
         for i, tok_major in enumerate((cos_tok, sin_tok)):
-            tb = psum.tile([P, TOK], F32, name="tb_ps", tag="mx", bufs=3)
+            tb = psum.tile([P, TOK], F32, name="tb_ps", tag=("tb0", "tb1")[i], bufs=1)
             for t in range(TT):
                 nc.tensor.transpose(tb[:, t * P : (t + 1) * P], tok_major[:, t * P : (t + 1) * P], ident[:])
             tb_ps.append(tb)
@@ -166,7 +186,7 @@ def tile_causalselfattention_pa_kernel(tc, x, freqs, Wq, bq, Wk, bk, gq, gk, out
         def x_transposes(c):
             xw = xraw[c][:].bitcast(F32)
             for h in range(2):
-                tag, bufs = (("to", 3), ("ta", 2))[h]
+                tag, bufs = (("mx", 3), ("ta", 2))[h]
                 xt = psum.tile([P, 2, 2, P], F32, name="xt", tag=tag, bufs=bufs)
                 for a in range(2):
                     for u in range(2):
@@ -196,33 +216,37 @@ def tile_causalselfattention_pa_kernel(tc, x, freqs, Wq, bq, Wk, bk, gq, gk, out
         load_unit(4)
         x_copies(0)
         load_unit(5)
-        copy_unit(1, v_cols(-1))
+        copy_unit(1, shares(-2))
         load_unit(6)
         x_transposes(1)
         x_quant(0)
         quant_unit(0)
         x_copies(1)
         load_unit(7)
-        copy_unit(2, v_cols(-1))
+        copy_unit(2, shares(-2))
         load_unit(8)
         x_transposes(2)
         x_quant(1)
         quant_unit(1)
         x_copies(2)
         load_unit(9)
-        copy_unit(3, v_cols(-1))
+        copy_unit(3, shares(-2))
         load_unit(10)
         x_transposes(3)
         x_quant(2)
         quant_unit(2)
         x_copies(3)
         load_unit(11)
-        copy_unit(4, v_cols(-1))
+        copy_unit(4, shares(-2))
         load_unit(12)
         x_quant(3)
         quant_unit(3)
-        copy_unit(5, v_cols(-1))
+        copy_unit(5, shares(-2))
         load_unit(13)
+        copy_unit(6, shares(-1))
+        load_unit(14)
+        copy_unit(7, shares(-1))
+        load_unit(15)
 
         ssp = const.tile([P, 2, TT, NCHUNK], F32, name="ssp")
         rstd = const.tile([P, 2, TT], F32, name="rstd")
@@ -247,6 +271,15 @@ def tile_causalselfattention_pa_kernel(tc, x, freqs, Wq, bq, Wk, bk, gq, gk, out
             a = work.tile([P, TOK], F32, name="a", tag="a", bufs=16)
             nc.scalar.activation(out=a[:], in_=acc[:], func=ACT.Identity, bias=prm[:, s : s + 1], scale=1.0)
             a_tiles[s] = a
+
+        def rope_tile_psum(s):
+            pr = work.tile([P, 2, TOK], F32, name="pr", tag="pr", bufs=PR_BUFS)
+            for i in range(2):
+                nc.vector.scalar_tensor_tensor(
+                    out=pr[:, i, :], in0=a_tiles[s][:], scalar=prm[:, 32 + s : 33 + s], in1=tb_ps[i][:],
+                    op0=ALU.mult, op1=ALU.mult,
+                )
+            p_tiles[s] = pr
 
         def rope_tile(s):
             pr = work.tile([P, 2, TOK], F32, name="pr", tag="pr", bufs=PR_BUFS)
@@ -312,7 +345,7 @@ def tile_causalselfattention_pa_kernel(tc, x, freqs, Wq, bq, Wk, bk, gq, gk, out
         pend_sq = []
         pend_out = []
         next_fq = 0
-        next_rk = NTILE // 2
+        next_rk = 2 * LAST_WINDOW
         for r in range(NROUND):
             acc0 = mx_tile(2 * r)
             acc1 = mx_tile(2 * r + 1)
@@ -325,15 +358,18 @@ def tile_causalselfattention_pa_kernel(tc, x, freqs, Wq, bq, Wk, bk, gq, gk, out
             for j in pend_out:
                 out_store(j, False)
             pend_out = []
-            if 1 <= r <= NROUND // 2:
-                rope_tile(2 * r - 2)
-                rope_tile(2 * r - 1)
-            for i in range(RK.get(r, 0)):
-                rope_tile(next_rk)
-                next_rk += 1
             if 2 * r + 5 < NUNIT:
                 quant_unit(2 * r + 4)
                 quant_unit(2 * r + 5)
+            if 2 * r + 9 < NUNIT:
+                copy_g(2 * r + 8, shares(r))
+                copy_g(2 * r + 9, shares(r))
+            if 1 <= r <= LAST_WINDOW:
+                rope_tile_psum(2 * r - 2)
+                rope_tile_psum(2 * r - 1)
+            for i in range(RK.get(r, 0)):
+                rope_tile(next_rk)
+                next_rk += 1
             bias_tile(2 * r, acc0)
             bias_tile(2 * r + 1, acc1)
             if q_done:
@@ -344,20 +380,20 @@ def tile_causalselfattention_pa_kernel(tc, x, freqs, Wq, bq, Wk, bk, gq, gk, out
                     sq_transposes(g, t, "ta", 2)
                     pend_sq.append((g, t))
             for i in range(FQ.get(r, 0)):
-                out_transposes(next_fq, "to", 3)
+                out_transposes(next_fq, ("to", "tb0", "tb1")[next_fq % 3], 1)
                 pend_out.append(next_fq)
                 next_fq += 1
-            if 2 * r + 7 < NUNIT:
-                copy_unit(2 * r + 6, v_cols(r))
-                copy_unit(2 * r + 7, v_cols(r))
+            if 2 * r + 9 < NUNIT:
+                copy_vs(2 * r + 8, shares(r))
+                copy_vs(2 * r + 9, shares(r))
             if q_done:
                 norm_recip(0)
-            if 2 * r + 15 < NUNIT:
-                load_unit(2 * r + 14)
-                load_unit(2 * r + 15)
+            if 2 * r + 17 < NUNIT:
+                load_unit(2 * r + 16)
+                load_unit(2 * r + 17)
 
         for i, t in enumerate(range(TT)):
-            tag, bufs = (("mx", 3), ("mx", 3), ("mx", 3), ("to", 3))[i]
+            tag, bufs = (("mx", 3), ("mx", 3), ("mx", 3), ("to", 1))[i]
             sq_transposes(NG - 1, t, tag, bufs)
         for g, t in pend_sq:
             sq_sum(g, t)
@@ -381,7 +417,7 @@ def tile_causalselfattention_pa_kernel(tc, x, freqs, Wq, bq, Wk, bk, gq, gk, out
             while next_rk < min(need, NTILE):
                 rope_tile(next_rk)
                 next_rk += 1
-            tag, bufs = (("ta", 2), ("to", 3), ("mx", 3))[k % 3]
+            tag, bufs = (("ta", 2), ("tb0", 1), ("mx", 3), ("ta", 2), ("tb1", 1), ("mx", 3), ("to", 1), ("mx", 3))[k % 8]
             out_transposes(j, tag, bufs)
             pend.append(j)
             k += 1

@@ -38,12 +38,12 @@ def shares(r):
     if r < 1:
         return (216, 0)
     if r < 5:
-        return (112, GC)
+        return (96, GC)
     if r <= LAST_WINDOW:
-        return (256, GC)
+        return (240, GC)
     return (360, 0)
 
-GC = 160
+GC = 176
 LAST_WINDOW = 9
 PR_BUFS = 20
 ST_BUFS = 6
@@ -159,8 +159,6 @@ def tile_causalselfattention_pa_kernel(tc, x, freqs, Wq, bq, Wk, bk, gq, gk, out
         )
         cos_tok = setup.tile([P, TT * P], F32, name="cos_tok")
         nc.scalar.activation(out=cos_tok[:], in_=cosarg[:], func=ACT.Sin)
-        prm_f = setup.tile([P, P], F32, name="prm_f")
-        nc.vector.tensor_copy(out=prm_f[:], in_=prm_raw[:])
         warm_in = setup.tile([P, 1], F32, name="warm_in")
         nc.vector.memset(warm_in[:], 1.0)
         warm_out = setup.tile([P, 1], F32, name="warm_out")
@@ -168,15 +166,6 @@ def tile_causalselfattention_pa_kernel(tc, x, freqs, Wq, bq, Wk, bk, gq, gk, out
 
         copy_unit(0, shares(-2))
 
-        prm_ps = psum.tile([P, 4 * P], F32, name="prm_ps", tag="mx", bufs=3)
-        nc.tensor.transpose(prm_ps[:, 0:P], prm_f[:], ident[:])
-        tables = const.tile([P, 2, TOK], F32, name="tables")
-        tb_ps = []
-        for i, tok_major in enumerate((cos_tok, sin_tok)):
-            tb = psum.tile([P, TOK], F32, name="tb_ps", tag=("tb0", "tb1")[i], bufs=1)
-            for t in range(TT):
-                nc.tensor.transpose(tb[:, t * P : (t + 1) * P], tok_major[:, t * P : (t + 1) * P], ident[:])
-            tb_ps.append(tb)
 
         xcodes = const.tile([P, PASSES, TOK], U32, name="xcodes", align_bytes=64)
         xscales = const.tile([P, PASSES, TOK], U8, name="xscales", align_bytes=64)
@@ -210,9 +199,6 @@ def tile_causalselfattention_pa_kernel(tc, x, freqs, Wq, bq, Wk, bk, gq, gk, out
 
         prm = const.tile([P, P], F32, name="prm")
         x_transposes(0)
-        nc.vector.tensor_copy(out=prm[:], in_=prm_ps[:, 0:P])
-        nc.vector.tensor_copy(out=tables[:, 0, :], in_=tb_ps[0][:])
-        nc.scalar.copy(out=tables[:, 1, :], in_=tb_ps[1][:])
         load_unit(4)
         x_copies(0)
         load_unit(5)
@@ -222,13 +208,27 @@ def tile_causalselfattention_pa_kernel(tc, x, freqs, Wq, bq, Wk, bk, gq, gk, out
         x_quant(0)
         quant_unit(0)
         x_copies(1)
+        prm_f = setup.tile([P, P], F32, name="prm_f")
+        nc.vector.tensor_copy(out=prm_f[:], in_=prm_raw[:])
         load_unit(7)
         copy_unit(2, shares(-2))
         load_unit(8)
         x_transposes(2)
+        prm_ps = psum.tile([P, 4 * P], F32, name="prm_ps", tag="mx", bufs=3)
+        nc.tensor.transpose(prm_ps[:, 0:P], prm_f[:], ident[:])
+        tables = const.tile([P, 2, TOK], F32, name="tables")
+        tb_ps = []
+        for i, tok_major in enumerate((cos_tok, sin_tok)):
+            tb = psum.tile([P, TOK], F32, name="tb_ps", tag=("tb0", "tb1")[i], bufs=1)
+            for t in range(TT):
+                nc.tensor.transpose(tb[:, t * P : (t + 1) * P], tok_major[:, t * P : (t + 1) * P], ident[:])
+            tb_ps.append(tb)
         x_quant(1)
         quant_unit(1)
         x_copies(2)
+        nc.vector.tensor_copy(out=prm[:], in_=prm_ps[:, 0:P])
+        nc.vector.tensor_copy(out=tables[:, 0, :], in_=tb_ps[0][:])
+        nc.scalar.copy(out=tables[:, 1, :], in_=tb_ps[1][:])
         load_unit(9)
         copy_unit(3, shares(-2))
         load_unit(10)

@@ -34,13 +34,13 @@ FLOPS = 2 * TOK * DIM * 2 * DQ
 
 def shares(r):
     if r < -1:
-        return (256, 0)
+        return (240, 0)
     if r < 1:
-        return (216, 0)
+        return (200, 0)
     if r < 5:
-        return (96, GC)
+        return (80, GC)
     if r <= LAST_WINDOW:
-        return (240, GC)
+        return (224, GC)
     return (360, 0)
 
 GC = 176
@@ -52,6 +52,19 @@ RK = {9: 0, 10: 0, 11: 0, 12: 1, 13: 3, 14: 4, 15: 4}
 TAIL_R = 6
 DEPTH = 4
 TAIL_FV = 2
+QV = 12
+
+
+def sq_plan(r):
+    if r < 2 or r == QN + 1:
+        return []
+    if r == QN:
+        return [(3, 0, "ta", 2), (3, 1, "ta", 2), (3, 2, "to", 1), (3, 3, "mx", 3)]
+    g = (r - 2) // 2
+    return [(g, 2 * (r % 2), "ta", 2), (g, 2 * (r % 2) + 1, "ta", 2)]
+
+
+QN = 8
 
 
 def tile_causalselfattention_pa_kernel(tc, x, freqs, Wq, bq, Wk, bk, gq, gk, out_0, out_1):
@@ -353,14 +366,14 @@ def tile_causalselfattention_pa_kernel(tc, x, freqs, Wq, bq, Wk, bk, gq, gk, out
             for g, t in pend_sq:
                 sq_sum(g, t)
             pend_sq = []
-            if q_done:
-                norm_mean(0)
             for j in pend_out:
-                out_store(j, False)
+                out_store(j, j >= QV)
             pend_out = []
             if 2 * r + 5 < NUNIT:
                 quant_unit(2 * r + 4)
                 quant_unit(2 * r + 5)
+            if q_done:
+                norm_mean(0)
             if 2 * r + 9 < NUNIT:
                 copy_g(2 * r + 8, shares(r))
                 copy_g(2 * r + 9, shares(r))
@@ -374,11 +387,9 @@ def tile_causalselfattention_pa_kernel(tc, x, freqs, Wq, bq, Wk, bk, gq, gk, out
             bias_tile(2 * r + 1, acc1)
             if q_done:
                 norm_sqrt(0)
-            if r >= 2:
-                g = (r - 2) // 2
-                for t in (2 * (r % 2), 2 * (r % 2) + 1):
-                    sq_transposes(g, t, "ta", 2)
-                    pend_sq.append((g, t))
+            for g, t, tag, bufs in sq_plan(r):
+                sq_transposes(g, t, tag, bufs)
+                pend_sq.append((g, t))
             for i in range(FQ.get(r, 0)):
                 out_transposes(next_fq, ("to", "tb0", "tb1")[next_fq % 3], 1)
                 pend_out.append(next_fq)
@@ -399,7 +410,7 @@ def tile_causalselfattention_pa_kernel(tc, x, freqs, Wq, bq, Wk, bk, gq, gk, out
             sq_sum(g, t)
         late = 0
         for j in pend_out:
-            out_store(j, False, late)
+            out_store(j, j >= QV, late)
             late += 1
         for i in range(TAIL_R):
             if next_rk < NTILE:

@@ -37,34 +37,18 @@ def shares(r):
         return (240, 0)
     if r < 1:
         return (200, 0)
-    if r < 5:
-        return (80, GC)
-    if r <= LAST_WINDOW:
-        return (224, GC)
-    return (360, 0)
+    return (VC, 0)
 
-GC = 176
-LAST_WINDOW = 9
-PR_BUFS = 20
+VC = 448
+A_BUFS = 32
+PS_BUFS = 6
+PR_BUFS = 16
 ST_BUFS = 6
-FQ = {10: 2, 11: 2, 12: 2, 13: 3, 14: 3, 15: 3}
-RK = {9: 0, 10: 0, 11: 0, 12: 1, 13: 3, 14: 4, 15: 4}
-TAIL_R = 6
-DEPTH = 4
-TAIL_FV = 2
-QV = 12
-
-
-def sq_plan(r):
-    if r < 2 or r == QN + 1:
-        return []
-    if r == QN:
-        return [(3, 0, "ta", 2), (3, 1, "ta", 2), (3, 2, "to", 1), (3, 3, "mx", 3)]
-    g = (r - 2) // 2
-    return [(g, 2 * (r % 2), "ta", 2), (g, 2 * (r % 2) + 1, "ta", 2)]
-
-
-QN = 8
+LAST_Q_ROUND = 12
+GT = (7, 11, 15, 19, 22, 23, 27)
+TILES_IN = {12: (0, 1), 13: (2, 3), 14: (4, 5, 6, 7), 15: (8, 9, 10, 11)}
+UNITS_IN = {14: (0, 1, 2, 3), 15: (4, 5, 6, 7)}
+FV = ()
 
 
 def tile_causalselfattention_pa_kernel(tc, x, freqs, Wq, bq, Wk, bk, gq, gk, out_0, out_1):
@@ -158,19 +142,19 @@ def tile_causalselfattention_pa_kernel(tc, x, freqs, Wq, bq, Wk, bk, gq, gk, out
         nc.vector.tensor_copy(out=swv[:, :, 0:1], in_=idv[:, :, 1:2])
         nc.vector.tensor_copy(out=swv[:, :, 1:2], in_=idv[:, :, 0:1])
 
-        ang = setup.tile([P, TT, HP, 2], F32, name="ang")
+        ang = work.tile([P, TT, HP, 2], F32, name="ang", tag="a", bufs=A_BUFS)
         nc.vector.tensor_copy(out=ang[:, :, :, 0], in_=fr_raw[:])
         nc.vector.tensor_scalar(out=ang[:, :, :, 1], in0=fr_raw[:], scalar1=-1.0, scalar2=None, op0=ALU.mult)
         angf = ang[:].rearrange("p t j e -> p (t j e)")
-        absang = setup.tile([P, TT * P], F32, name="absang")
+        absang = work.tile([P, TT * P], F32, name="absang", tag="a", bufs=A_BUFS)
         nc.scalar.activation(out=absang[:], in_=angf, func=ACT.Abs)
-        sin_tok = setup.tile([P, TT * P], F32, name="sin_tok")
+        sin_tok = work.tile([P, TT * P], F32, name="sin_tok", tag="a", bufs=A_BUFS)
         nc.scalar.activation(out=sin_tok[:], in_=angf, func=ACT.Sin)
-        cosarg = setup.tile([P, TT * P], F32, name="cosarg")
+        cosarg = work.tile([P, TT * P], F32, name="cosarg", tag="a", bufs=A_BUFS)
         nc.vector.tensor_scalar(
             out=cosarg[:], in0=absang[:], scalar1=-1.0, scalar2=HALF_PI, op0=ALU.mult, op1=ALU.add
         )
-        cos_tok = setup.tile([P, TT * P], F32, name="cos_tok")
+        cos_tok = work.tile([P, TT * P], F32, name="cos_tok", tag="a", bufs=A_BUFS)
         nc.scalar.activation(out=cos_tok[:], in_=cosarg[:], func=ACT.Sin)
         warm_in = setup.tile([P, 1], F32, name="warm_in")
         nc.vector.memset(warm_in[:], 1.0)
@@ -188,7 +172,7 @@ def tile_causalselfattention_pa_kernel(tc, x, freqs, Wq, bq, Wk, bk, gq, gk, out
         def x_transposes(c):
             xw = xraw[c][:].bitcast(F32)
             for h in range(2):
-                tag, bufs = (("mx", 3), ("ta", 2))[h]
+                tag, bufs = "ps", PS_BUFS
                 xt = psum.tile([P, 2, 2, P], F32, name="xt", tag=tag, bufs=bufs)
                 for a in range(2):
                     for u in range(2):
@@ -227,7 +211,7 @@ def tile_causalselfattention_pa_kernel(tc, x, freqs, Wq, bq, Wk, bk, gq, gk, out
         copy_unit(2, shares(-2))
         load_unit(8)
         x_transposes(2)
-        prm_ps = psum.tile([P, 4 * P], F32, name="prm_ps", tag="mx", bufs=3)
+        prm_ps = psum.tile([P, 4 * P], F32, name="prm_ps", tag="ps", bufs=PS_BUFS)
         nc.tensor.transpose(prm_ps[:, 0:P], prm_f[:], ident[:])
         tables = const.tile([P, 2, TOK], F32, name="tables")
         tb_ps = []
@@ -263,10 +247,11 @@ def tile_causalselfattention_pa_kernel(tc, x, freqs, Wq, bq, Wk, bk, gq, gk, out
 
         ssp = const.tile([P, 2, TT, NCHUNK], F32, name="ssp")
         rstd = const.tile([P, 2, TT], F32, name="rstd")
+        prmg = const.tile([P, NTILE], F32, name="prmg")
 
         def mx_tile(s):
             g, m = s // MT, s % MT
-            acc = psum.tile([P, TOK], F32, name="acc", tag="mx", bufs=3)
+            acc = psum.tile([P, TOK], F32, name="acc", tag="ps", bufs=PS_BUFS)
             for c in range(PASSES):
                 codes, scales = code_tiles[g * PASSES + c]
                 nc.tensor.matmul_mx(
@@ -281,11 +266,11 @@ def tile_causalselfattention_pa_kernel(tc, x, freqs, Wq, bq, Wk, bk, gq, gk, out
             return acc
 
         def bias_tile(s, acc):
-            a = work.tile([P, TOK], F32, name="a", tag="a", bufs=16)
+            a = work.tile([P, TOK], F32, name="a", tag="a", bufs=A_BUFS)
             nc.scalar.activation(out=a[:], in_=acc[:], func=ACT.Identity, bias=prm[:, s : s + 1], scale=1.0)
             a_tiles[s] = a
 
-        def rope_tile_psum(s):
+        def rope_v(s):
             pr = work.tile([P, 2, TOK], F32, name="pr", tag="pr", bufs=PR_BUFS)
             for i in range(2):
                 nc.vector.scalar_tensor_tensor(
@@ -294,24 +279,29 @@ def tile_causalselfattention_pa_kernel(tc, x, freqs, Wq, bq, Wk, bk, gq, gk, out
                 )
             p_tiles[s] = pr
 
-        def rope_tile(s):
-            pr = work.tile([P, 2, TOK], F32, name="pr", tag="pr", bufs=PR_BUFS)
-            nc.vector.scalar_tensor_tensor(
-                out=pr[:], in0=a_tiles[s][:].unsqueeze(1).to_broadcast([P, 2, TOK]),
-                scalar=prm[:, 32 + s : 33 + s], in1=tables[:], op0=ALU.mult, op1=ALU.mult,
+        def rope_g(s):
+            ag = work.tile([P, TOK], F32, name="ag", tag="ag", bufs=2)
+            nc.gpsimd.tensor_scalar(
+                out=ag[:], in0=a_tiles[s][:], scalar1=prmg[:, s : s + 1], scalar2=0.0, op0=ALU.mult, op1=ALU.add
             )
+            pr = work.tile([P, 2, TOK], F32, name="pr", tag="pr", bufs=PR_BUFS)
+            for i in range(2):
+                nc.gpsimd.tensor_tensor(out=pr[:, i, :], in0=ag[:], in1=tables[:, i, :], op=ALU.mult)
             p_tiles[s] = pr
 
-        def sq_transposes(g, t, tag, bufs):
-            ta = psum.tile([P, CHUNK], F32, name="ta", tag=tag, bufs=bufs)
+        def rope(s):
+            if s in GT:
+                rope_g(s)
+            else:
+                rope_v(s)
+
+        def sq_unit(g, t):
+            ta = psum.tile([P, CHUNK], F32, name="ta", tag="ps", bufs=PS_BUFS)
             for m in range(MT):
                 nc.tensor.transpose(ta[:, m * P : (m + 1) * P], a_tiles[g * MT + m][:, t * P : (t + 1) * P], ident[:])
-            ta_tiles[(g, t)] = ta
-
-        def sq_sum(g, t):
             junk = work.tile([P, CHUNK], F32, name="junk", tag="junk", bufs=2)
             nc.scalar.activation(
-                out=junk[:], in_=ta_tiles[(g, t)][:], func=ACT.Square,
+                out=junk[:], in_=ta[:], func=ACT.Square,
                 accum_out=ssp[:, g // NCHUNK, t, g % NCHUNK : g % NCHUNK + 1],
             )
 
@@ -322,120 +312,73 @@ def tile_causalselfattention_pa_kernel(tc, x, freqs, Wq, bq, Wk, bk, gq, gk, out
             nc.vector.tensor_scalar(
                 out=stat[:, mat, 1, :], in0=stat[:, mat, 0, :], scalar1=1.0 / DQ, scalar2=EPS, op0=ALU.mult, op1=ALU.add
             )
-
-        def norm_sqrt(mat):
             nc.scalar.activation(out=stat[:, mat, 2, :], in_=stat[:, mat, 1, :], func=ACT.Sqrt)
 
         def norm_recip(mat):
             nc.vector.reciprocal(out=rstd[:, mat, :], in_=stat[:, mat, 2, :])
 
-        def out_transposes(j, tag, bufs):
+        def out_unit(j):
             g, t = j // TT, j % TT
-            to = psum.tile([P, CHUNK], F32, name="to", tag=tag, bufs=bufs)
+            mat = g // NCHUNK
+            to = psum.tile([P, CHUNK], F32, name="to", tag="ps", bufs=PS_BUFS)
             for m in range(MT):
                 pr = p_tiles[g * MT + m]
                 dst = to[:, m * P : (m + 1) * P]
                 nc.tensor.matmul(dst, lhsT=pr[:, 0, t * P : (t + 1) * P], rhs=ident[:], is_transpose=True, start=True, stop=False)
                 nc.tensor.matmul(dst, lhsT=pr[:, 1, t * P : (t + 1) * P], rhs=swap[:], is_transpose=True, start=False, stop=True)
-            to_tiles[j] = to
-
-        def out_store(j, on_vector, late=0):
-            g, t = j // TT, j % TT
-            mat = g // NCHUNK
-            if late % 3 == 1:
+            if j % 3 == 1:
                 st = wpool.tile([P, CHUNK], F32, name="st", tag="raw", bufs=8)
-            elif late % 3 == 2:
+            elif j % 3 == 2:
                 st = wpool.tile([P, CHUNK], F32, name="st", tag="wg", bufs=4, align_bytes=64)
             else:
                 st = work.tile([P, CHUNK], F32, name="st", tag="st", bufs=ST_BUFS)
-            if on_vector:
-                nc.vector.tensor_scalar(out=st[:], in0=to_tiles[j][:], scalar1=rstd[:, mat, t : t + 1], scalar2=None, op0=ALU.mult)
+            if j in FV:
+                nc.vector.tensor_scalar(out=st[:], in0=to[:], scalar1=rstd[:, mat, t : t + 1], scalar2=None, op0=ALU.mult)
             else:
-                nc.scalar.activation(out=st[:], in_=to_tiles[j][:], func=ACT.Copy, scale=rstd[:, mat, t : t + 1])
+                nc.scalar.activation(out=st[:], in_=to[:], func=ACT.Copy, scale=rstd[:, mat, t : t + 1])
             n0 = (g % NCHUNK) * CHUNK
             nc.sync.dma_start(out=outs[mat][t * P : (t + 1) * P, n0 : n0 + CHUNK], in_=st[:])
 
-        pend_sq = []
-        pend_out = []
-        next_fq = 0
-        next_rk = 2 * LAST_WINDOW
         for r in range(NROUND):
             acc0 = mx_tile(2 * r)
             acc1 = mx_tile(2 * r + 1)
-            q_done = bool(pend_sq) and pend_sq[-1] == (NCHUNK - 1, TT - 1)
-            for g, t in pend_sq:
-                sq_sum(g, t)
-            pend_sq = []
-            for j in pend_out:
-                out_store(j, j >= QV)
-            pend_out = []
-            if 2 * r + 5 < NUNIT:
+            if r < LAST_Q_ROUND:
                 quant_unit(2 * r + 4)
                 quant_unit(2 * r + 5)
-            if q_done:
+            if r == LAST_Q_ROUND:
+                for u in range(2 * r + 4, NUNIT):
+                    quant_unit(u)
+                nc.vector.tensor_copy(out=prmg[:], in_=prm[:, 32 : 32 + NTILE])
                 norm_mean(0)
-            if 2 * r + 9 < NUNIT:
-                copy_g(2 * r + 8, shares(r))
-                copy_g(2 * r + 9, shares(r))
-            if 1 <= r <= LAST_WINDOW:
-                rope_tile_psum(2 * r - 2)
-                rope_tile_psum(2 * r - 1)
-            for i in range(RK.get(r, 0)):
-                rope_tile(next_rk)
-                next_rk += 1
+            first = True
+            for s in TILES_IN.get(r, ()):
+                rope(s)
+                if r == LAST_Q_ROUND and first:
+                    norm_recip(0)
+                first = False
             bias_tile(2 * r, acc0)
             bias_tile(2 * r + 1, acc1)
-            if q_done:
-                norm_sqrt(0)
-            for g, t, tag, bufs in sq_plan(r):
-                sq_transposes(g, t, tag, bufs)
-                pend_sq.append((g, t))
-            for i in range(FQ.get(r, 0)):
-                out_transposes(next_fq, ("to", "tb0", "tb1")[next_fq % 3], 1)
-                pend_out.append(next_fq)
-                next_fq += 1
+            if r >= 2:
+                sq_unit((r - 2) // 2, 2 * (r % 2))
+                sq_unit((r - 2) // 2, 2 * (r % 2) + 1)
+            for j in UNITS_IN.get(r, ()):
+                out_unit(j)
             if 2 * r + 9 < NUNIT:
-                copy_vs(2 * r + 8, shares(r))
-                copy_vs(2 * r + 9, shares(r))
-            if q_done:
-                norm_recip(0)
+                copy_unit(2 * r + 8, shares(r))
+                copy_unit(2 * r + 9, shares(r))
             if 2 * r + 17 < NUNIT:
                 load_unit(2 * r + 16)
                 load_unit(2 * r + 17)
 
-        for i, t in enumerate(range(TT)):
-            tag, bufs = (("mx", 3), ("mx", 3), ("mx", 3), ("to", 1))[i]
-            sq_transposes(NG - 1, t, tag, bufs)
-        for g, t in pend_sq:
-            sq_sum(g, t)
-        late = 0
-        for j in pend_out:
-            out_store(j, j >= QV, late)
-            late += 1
-        for i in range(TAIL_R):
-            if next_rk < NTILE:
-                rope_tile(next_rk)
-                next_rk += 1
         for t in range(TT):
-            sq_sum(NG - 1, t)
-        norm_mean(1)
-        norm_sqrt(1)
-        norm_recip(1)
-        pend = []
-        k = 0
-        for j in range(next_fq, NG * TT):
-            need = (j // TT) * MT + MT
-            while next_rk < min(need, NTILE):
-                rope_tile(next_rk)
-                next_rk += 1
-            tag, bufs = (("ta", 2), ("tb0", 1), ("mx", 3), ("ta", 2), ("tb1", 1), ("mx", 3), ("to", 1), ("mx", 3))[k % 8]
-            out_transposes(j, tag, bufs)
-            pend.append(j)
-            k += 1
-            if len(pend) > DEPTH:
-                out_store(pend[0], TAIL_FV > 0 and late % TAIL_FV == TAIL_FV - 1, late)
-                late += 1
-                pend = pend[1:]
-        for j in pend:
-            out_store(j, TAIL_FV > 0 and late % TAIL_FV == TAIL_FV - 1, late)
-            late += 1
+            sq_unit(NG - 1, t)
+        for g in range(3, NG + 1):
+            if g < NG:
+                for m in range(MT):
+                    rope(g * MT + m)
+                    if g == 4 and m == 0:
+                        norm_mean(1)
+                    if g == 4 and m == 1:
+                        norm_recip(1)
+            for t in range(TT):
+                out_unit((g - 1) * TT + t)

@@ -32,11 +32,13 @@ NROUND = NTILE // 2
 
 FLOPS = 2 * TOK * DIM * 2 * DQ
 
-def shares(r):
-    if r < -1:
-        return (240, 0)
-    if r < 1:
-        return (200, 0)
+def shares(u):
+    if u < 4:
+        return (304, 0)
+    if u < 8:
+        return (256, 0)
+    if u < 12:
+        return (352, 0)
     return (VC, 0)
 
 VC = 448
@@ -45,10 +47,13 @@ PS_BUFS = 6
 PR_BUFS = 16
 ST_BUFS = 6
 LAST_Q_ROUND = 12
-GT = (7, 11, 15, 19, 22, 23, 27)
+TABLES_ROUND = 10
+GT = (7, 11, 14, 15, 19, 23, 26, 27)
+AG_IN = {12: (7,), 13: (11,), 14: (14, 15), 15: (19,)}
+AG_IN2 = {3: (23,), 4: (26, 27)}
 TILES_IN = {12: (0, 1), 13: (2, 3), 14: (4, 5, 6, 7), 15: (8, 9, 10, 11)}
 UNITS_IN = {14: (0, 1, 2, 3), 15: (4, 5, 6, 7)}
-FV = ()
+FV = (29, 31)
 
 
 def tile_causalselfattention_pa_kernel(tc, x, freqs, Wq, bq, Wk, bk, gq, gk, out_0, out_1):
@@ -122,6 +127,10 @@ def tile_causalselfattention_pa_kernel(tc, x, freqs, Wq, bq, Wk, bk, gq, gk, out
 
         prm_raw = setup.tile([P, P], BF16, name="prm_raw")
         nc.vector.memset(prm_raw[:], 0.0)
+        warm_in = setup.tile([P, 1], F32, name="warm_in")
+        nc.vector.memset(warm_in[:], 1.0)
+        minus_half = const.tile([P, TT], F32, name="minus_half")
+        nc.vector.memset(minus_half[:], -0.5)
         fr_raw = setup.tile([P, TT, HP], BF16, name="fr_raw")
         nc.scalar.dma_start(out=fr_raw[:], in_=freqs.rearrange("(t p) j -> p t j", p=P))
         for v, vec in enumerate((bq, bk, gq, gk)):
@@ -142,27 +151,21 @@ def tile_causalselfattention_pa_kernel(tc, x, freqs, Wq, bq, Wk, bk, gq, gk, out
         nc.vector.tensor_copy(out=swv[:, :, 0:1], in_=idv[:, :, 1:2])
         nc.vector.tensor_copy(out=swv[:, :, 1:2], in_=idv[:, :, 0:1])
 
-        ang = work.tile([P, TT, HP, 2], F32, name="ang", tag="a", bufs=A_BUFS)
-        nc.vector.tensor_copy(out=ang[:, :, :, 0], in_=fr_raw[:])
-        nc.vector.tensor_scalar(out=ang[:, :, :, 1], in0=fr_raw[:], scalar1=-1.0, scalar2=None, op0=ALU.mult)
-        angf = ang[:].rearrange("p t j e -> p (t j e)")
-        absang = work.tile([P, TT * P], F32, name="absang", tag="a", bufs=A_BUFS)
-        nc.scalar.activation(out=absang[:], in_=angf, func=ACT.Abs)
-        sin_tok = work.tile([P, TT * P], F32, name="sin_tok", tag="a", bufs=A_BUFS)
-        nc.scalar.activation(out=sin_tok[:], in_=angf, func=ACT.Sin)
-        cosarg = work.tile([P, TT * P], F32, name="cosarg", tag="a", bufs=A_BUFS)
-        nc.vector.tensor_scalar(
-            out=cosarg[:], in0=absang[:], scalar1=-1.0, scalar2=HALF_PI, op0=ALU.mult, op1=ALU.add
+        warm_out = setup.tile([P, 2], F32, name="warm_out")
+        nc.scalar.activation(out=warm_out[:, 0:1], in_=warm_in[:], func=ACT.Sin)
+
+        copy_unit(0, shares(0))
+        load_unit(4)
+
+        sin_tok = work.tile([P, TT, HP, 2], F32, name="sin_tok", tag="a", bufs=A_BUFS)
+        nc.scalar.activation(out=sin_tok[:, :, :, 0], in_=fr_raw[:], func=ACT.Sin)
+        nc.scalar.activation(out=sin_tok[:, :, :, 1], in_=fr_raw[:], func=ACT.Sin, scale=-1.0)
+        absf = work.tile([P, TT, HP], F32, name="absf", tag="a", bufs=A_BUFS)
+        nc.scalar.activation(out=absf[:], in_=fr_raw[:], func=ACT.Abs)
+        cos_tok = work.tile([P, TT, HP, 2], F32, name="cos_tok", tag="a", bufs=A_BUFS)
+        nc.scalar.activation(
+            out=cos_tok[:], in_=absf[:].unsqueeze(3).to_broadcast([P, TT, HP, 2]), func=ACT.Sin, scale=-1.0, bias=HALF_PI
         )
-        cos_tok = work.tile([P, TT * P], F32, name="cos_tok", tag="a", bufs=A_BUFS)
-        nc.scalar.activation(out=cos_tok[:], in_=cosarg[:], func=ACT.Sin)
-        warm_in = setup.tile([P, 1], F32, name="warm_in")
-        nc.vector.memset(warm_in[:], 1.0)
-        warm_out = setup.tile([P, 1], F32, name="warm_out")
-        nc.scalar.activation(out=warm_out[:], in_=warm_in[:], func=ACT.Sqrt)
-
-        copy_unit(0, shares(-2))
-
 
         xcodes = const.tile([P, PASSES, TOK], U32, name="xcodes", align_bytes=64)
         xscales = const.tile([P, PASSES, TOK], U8, name="xscales", align_bytes=64)
@@ -196,58 +199,50 @@ def tile_causalselfattention_pa_kernel(tc, x, freqs, Wq, bq, Wk, bk, gq, gk, out
 
         prm = const.tile([P, P], F32, name="prm")
         x_transposes(0)
-        load_unit(4)
-        x_copies(0)
         load_unit(5)
-        copy_unit(1, shares(-2))
-        load_unit(6)
-        x_transposes(1)
-        x_quant(0)
         quant_unit(0)
-        x_copies(1)
+        copy_unit(1, shares(1))
+        load_unit(6)
         prm_f = setup.tile([P, P], F32, name="prm_f")
         nc.vector.tensor_copy(out=prm_f[:], in_=prm_raw[:])
-        load_unit(7)
-        copy_unit(2, shares(-2))
-        load_unit(8)
-        x_transposes(2)
         prm_ps = psum.tile([P, 4 * P], F32, name="prm_ps", tag="ps", bufs=PS_BUFS)
         nc.tensor.transpose(prm_ps[:, 0:P], prm_f[:], ident[:])
-        tables = const.tile([P, 2, TOK], F32, name="tables")
+        x_copies(0)
+        x_transposes(1)
+        load_unit(7)
+        quant_unit(1)
+        x_quant(0)
+        nc.vector.tensor_copy(out=prm[:], in_=prm_ps[:, 0:P])
+        copy_unit(2, shares(2))
+        load_unit(8)
+        x_copies(1)
+        x_transposes(2)
+        load_unit(9)
+        quant_unit(2)
+        x_quant(1)
+        copy_unit(3, shares(3))
+        load_unit(10)
+        x_copies(2)
+        x_transposes(3)
+        load_unit(11)
         tb_ps = []
         for i, tok_major in enumerate((cos_tok, sin_tok)):
             tb = psum.tile([P, TOK], F32, name="tb_ps", tag=("tb0", "tb1")[i], bufs=1)
+            tmv = tok_major[:].rearrange("p t j e -> p (t j e)")
             for t in range(TT):
-                nc.tensor.transpose(tb[:, t * P : (t + 1) * P], tok_major[:, t * P : (t + 1) * P], ident[:])
+                nc.tensor.transpose(tb[:, t * P : (t + 1) * P], tmv[:, t * P : (t + 1) * P], ident[:])
             tb_ps.append(tb)
-        x_quant(1)
-        quant_unit(1)
-        x_copies(2)
-        nc.vector.tensor_copy(out=prm[:], in_=prm_ps[:, 0:P])
-        nc.vector.tensor_copy(out=tables[:, 0, :], in_=tb_ps[0][:])
-        nc.scalar.copy(out=tables[:, 1, :], in_=tb_ps[1][:])
-        load_unit(9)
-        copy_unit(3, shares(-2))
-        load_unit(10)
-        x_transposes(3)
-        x_quant(2)
-        quant_unit(2)
-        x_copies(3)
-        load_unit(11)
-        copy_unit(4, shares(-2))
-        load_unit(12)
-        x_quant(3)
         quant_unit(3)
-        copy_unit(5, shares(-2))
-        load_unit(13)
-        copy_unit(6, shares(-1))
-        load_unit(14)
-        copy_unit(7, shares(-1))
-        load_unit(15)
+        x_quant(2)
+        x_copies(3)
+        x_quant(3)
+        for u in range(4, 8):
+            copy_unit(u, shares(u))
+            load_unit(u + 8)
+        tables = const.tile([P, 2, TOK], F32, name="tables")
 
         ssp = const.tile([P, 2, TT, NCHUNK], F32, name="ssp")
         rstd = const.tile([P, 2, TT], F32, name="rstd")
-        prmg = const.tile([P, NTILE], F32, name="prmg")
 
         def mx_tile(s):
             g, m = s // MT, s % MT
@@ -279,11 +274,28 @@ def tile_causalselfattention_pa_kernel(tc, x, freqs, Wq, bq, Wk, bk, gq, gk, out
                 )
             p_tiles[s] = pr
 
+        def rope_last_chunk():
+            for m in range(MT):
+                p_tiles[(NG - 1) * MT + m] = work.tile([P, 2, TOK], F32, name="pr", tag="pr", bufs=PR_BUFS)
+            for h in range(2):
+                cols = slice(h * (TOK // 2), (h + 1) * (TOK // 2))
+                for m in range(MT):
+                    s = (NG - 1) * MT + m
+                    for i in range(2):
+                        nc.vector.scalar_tensor_tensor(
+                            out=p_tiles[s][:, i, cols], in0=a_tiles[s][:, cols], scalar=prm[:, 32 + s : 33 + s],
+                            in1=tb_ps[i][:, cols], op0=ALU.mult, op1=ALU.mult,
+                        )
+
+        ag_tiles = {}
+
+        def gain_tile(s):
+            ag = work.tile([P, TOK], F32, name="ag", tag="ag", bufs=8)
+            nc.scalar.activation(out=ag[:], in_=a_tiles[s][:], func=ACT.Copy, scale=prm[:, 32 + s : 33 + s])
+            ag_tiles[s] = ag
+
         def rope_g(s):
-            ag = work.tile([P, TOK], F32, name="ag", tag="ag", bufs=2)
-            nc.gpsimd.tensor_scalar(
-                out=ag[:], in0=a_tiles[s][:], scalar1=prmg[:, s : s + 1], scalar2=0.0, op0=ALU.mult, op1=ALU.add
-            )
+            ag = ag_tiles[s]
             pr = work.tile([P, 2, TOK], F32, name="pr", tag="pr", bufs=PR_BUFS)
             for i in range(2):
                 nc.gpsimd.tensor_tensor(out=pr[:, i, :], in0=ag[:], in1=tables[:, i, :], op=ALU.mult)
@@ -312,10 +324,9 @@ def tile_causalselfattention_pa_kernel(tc, x, freqs, Wq, bq, Wk, bk, gq, gk, out
             nc.vector.tensor_scalar(
                 out=stat[:, mat, 1, :], in0=stat[:, mat, 0, :], scalar1=1.0 / DQ, scalar2=EPS, op0=ALU.mult, op1=ALU.add
             )
-            nc.scalar.activation(out=stat[:, mat, 2, :], in_=stat[:, mat, 1, :], func=ACT.Sqrt)
 
-        def norm_recip(mat):
-            nc.vector.reciprocal(out=rstd[:, mat, :], in_=stat[:, mat, 2, :])
+        def norm_power(mat):
+            nc.gpsimd.tensor_tensor(out=rstd[:, mat, :], in0=stat[:, mat, 1, :], in1=minus_half[:], op=ALU.pow)
 
         def out_unit(j):
             g, t = j // TT, j % TT
@@ -326,12 +337,10 @@ def tile_causalselfattention_pa_kernel(tc, x, freqs, Wq, bq, Wk, bk, gq, gk, out
                 dst = to[:, m * P : (m + 1) * P]
                 nc.tensor.matmul(dst, lhsT=pr[:, 0, t * P : (t + 1) * P], rhs=ident[:], is_transpose=True, start=True, stop=False)
                 nc.tensor.matmul(dst, lhsT=pr[:, 1, t * P : (t + 1) * P], rhs=swap[:], is_transpose=True, start=False, stop=True)
-            if j % 3 == 1:
-                st = wpool.tile([P, CHUNK], F32, name="st", tag="raw", bufs=8)
-            elif j % 3 == 2:
+            if j % 3 == 2:
                 st = wpool.tile([P, CHUNK], F32, name="st", tag="wg", bufs=4, align_bytes=64)
             else:
-                st = work.tile([P, CHUNK], F32, name="st", tag="st", bufs=ST_BUFS)
+                st = wpool.tile([P, CHUNK], F32, name="st", tag="raw", bufs=8)
             if j in FV:
                 nc.vector.tensor_scalar(out=st[:], in0=to[:], scalar1=rstd[:, mat, t : t + 1], scalar2=None, op0=ALU.mult)
             else:
@@ -342,20 +351,24 @@ def tile_causalselfattention_pa_kernel(tc, x, freqs, Wq, bq, Wk, bk, gq, gk, out
         for r in range(NROUND):
             acc0 = mx_tile(2 * r)
             acc1 = mx_tile(2 * r + 1)
-            if r < LAST_Q_ROUND:
+            if r == 0:
+                for u in range(4, 8):
+                    quant_unit(u)
+            if 2 <= r < LAST_Q_ROUND:
                 quant_unit(2 * r + 4)
                 quant_unit(2 * r + 5)
+            if r == TABLES_ROUND:
+                nc.vector.tensor_copy(out=tables[:, 0, :], in_=tb_ps[0][:])
+                nc.scalar.copy(out=tables[:, 1, :], in_=tb_ps[1][:])
             if r == LAST_Q_ROUND:
                 for u in range(2 * r + 4, NUNIT):
                     quant_unit(u)
-                nc.vector.tensor_copy(out=prmg[:], in_=prm[:, 32 : 32 + NTILE])
                 norm_mean(0)
-            first = True
+                norm_power(0)
+            for s in AG_IN.get(r, ()):
+                gain_tile(s)
             for s in TILES_IN.get(r, ()):
                 rope(s)
-                if r == LAST_Q_ROUND and first:
-                    norm_recip(0)
-                first = False
             bias_tile(2 * r, acc0)
             bias_tile(2 * r + 1, acc1)
             if r >= 2:
@@ -364,8 +377,8 @@ def tile_causalselfattention_pa_kernel(tc, x, freqs, Wq, bq, Wk, bk, gq, gk, out
             for j in UNITS_IN.get(r, ()):
                 out_unit(j)
             if 2 * r + 9 < NUNIT:
-                copy_unit(2 * r + 8, shares(r))
-                copy_unit(2 * r + 9, shares(r))
+                copy_unit(2 * r + 8, shares(2 * r + 8))
+                copy_unit(2 * r + 9, shares(2 * r + 9))
             if 2 * r + 17 < NUNIT:
                 load_unit(2 * r + 16)
                 load_unit(2 * r + 17)
@@ -373,12 +386,16 @@ def tile_causalselfattention_pa_kernel(tc, x, freqs, Wq, bq, Wk, bk, gq, gk, out
         for t in range(TT):
             sq_unit(NG - 1, t)
         for g in range(3, NG + 1):
-            if g < NG:
+            for s in AG_IN2.get(g, ()):
+                gain_tile(s)
+            if g == NG - 1:
+                rope_last_chunk()
+            elif g < NG:
                 for m in range(MT):
                     rope(g * MT + m)
-                    if g == 4 and m == 0:
+                    if g == 4 and m == 2:
                         norm_mean(1)
-                    if g == 4 and m == 1:
-                        norm_recip(1)
+                    if g == 5 and m == 3:
+                        norm_power(1)
             for t in range(TT):
                 out_unit((g - 1) * TT + t)

@@ -52,7 +52,7 @@ GT = (7, 11, 14, 15, 19, 23, 26, 27)
 AG_IN = {12: (7,), 13: (11,), 14: (14, 15), 15: (19,)}
 AG_IN2 = {3: (23,), 4: (26, 27)}
 TILES_IN = {12: (0, 1), 13: (2, 3), 14: (4, 5, 6, 7), 15: (8, 9, 10, 11)}
-UNITS_IN = {14: (0, 1, 2, 3), 15: (4, 5, 6, 7)}
+UNITS_IN = {15: (0, 1, 2, 3)}
 FV = (29, 31)
 
 
@@ -371,9 +371,9 @@ def tile_causalselfattention_pa_kernel(tc, x, freqs, Wq, bq, Wk, bk, gq, gk, out
                 rope(s)
             bias_tile(2 * r, acc0)
             bias_tile(2 * r + 1, acc1)
-            if r >= 2:
-                sq_unit((r - 2) // 2, 2 * (r % 2))
-                sq_unit((r - 2) // 2, 2 * (r % 2) + 1)
+            if r >= 3 and r % 2 == 1:
+                for t in range(TT):
+                    sq_unit((r - 3) // 2, t)
             for j in UNITS_IN.get(r, ()):
                 out_unit(j)
             if 2 * r + 9 < NUNIT:
@@ -385,6 +385,8 @@ def tile_causalselfattention_pa_kernel(tc, x, freqs, Wq, bq, Wk, bk, gq, gk, out
 
         for t in range(TT):
             sq_unit(NG - 1, t)
+        for j in range(TT, 2 * TT):
+            out_unit(j)
         for g in range(3, NG + 1):
             for s in AG_IN2.get(g, ()):
                 gain_tile(s)

@@ -127,6 +127,7 @@ def tile_causalselfattention_pa_kernel(tc, x, freqs, Wq, bq, Wk, bk, gq, gk, out
 
         prm_raw = setup.tile([P, P], BF16, name="prm_raw")
         nc.vector.memset(prm_raw[:], 0.0)
+        nc.vector.memset(prm_raw[96:P, :], 1.0)
         warm_in = setup.tile([P, 1], F32, name="warm_in")
         nc.vector.memset(warm_in[:], 1.0)
         minus_half = const.tile([P, TT], F32, name="minus_half")
@@ -136,12 +137,21 @@ def tile_causalselfattention_pa_kernel(tc, x, freqs, Wq, bq, Wk, bk, gq, gk, out
         for v, vec in enumerate((bq, bk, gq, gk)):
             nc.scalar.dma_start(out=prm_raw[16 * v : 16 * v + 16, :], in_=vec.rearrange("(m p) -> m p", p=P))
         xv = x.rearrange("b (t p) k -> p (b t) k", p=P)
-        xraw = []
-        for c in range(PASSES):
-            load_unit(c)
+        xraw = {}
+
+        def load_x(c):
             xr = wpool.tile([P, TT, K_PASS], BF16, name="xraw", tag="raw", bufs=8)
             nc.sync.dma_start(out=xr[:], in_=xv[:, :, c * K_PASS : (c + 1) * K_PASS])
-            xraw.append(xr)
+            xraw[c] = xr
+
+        load_unit(0)
+        load_x(0)
+        load_x(1)
+        load_unit(1)
+        load_x(2)
+        load_unit(2)
+        load_x(3)
+        load_unit(3)
 
         ident = const.tile([P, P], F32, name="ident")
         make_identity(nc, ident[:])
@@ -158,8 +168,7 @@ def tile_causalselfattention_pa_kernel(tc, x, freqs, Wq, bq, Wk, bk, gq, gk, out
         load_unit(4)
 
         sin_tok = work.tile([P, TT, HP, 2], F32, name="sin_tok", tag="a", bufs=A_BUFS)
-        nc.scalar.activation(out=sin_tok[:, :, :, 0], in_=fr_raw[:], func=ACT.Sin)
-        nc.scalar.activation(out=sin_tok[:, :, :, 1], in_=fr_raw[:], func=ACT.Sin, scale=-1.0)
+        nc.scalar.activation(out=sin_tok[:], in_=fr_raw[:].unsqueeze(3).to_broadcast([P, TT, HP, 2]), func=ACT.Sin)
         absf = work.tile([P, TT, HP], F32, name="absf", tag="a", bufs=A_BUFS)
         nc.scalar.activation(out=absf[:], in_=fr_raw[:], func=ACT.Abs)
         cos_tok = work.tile([P, TT, HP, 2], F32, name="cos_tok", tag="a", bufs=A_BUFS)
@@ -201,30 +210,32 @@ def tile_causalselfattention_pa_kernel(tc, x, freqs, Wq, bq, Wk, bk, gq, gk, out
         x_transposes(0)
         load_unit(5)
         quant_unit(0)
-        copy_unit(1, shares(1))
+        x_copies(0)
+        x_transposes(1)
         load_unit(6)
         prm_f = setup.tile([P, P], F32, name="prm_f")
         nc.vector.tensor_copy(out=prm_f[:], in_=prm_raw[:])
+        odd = prm_f[96:P, :].rearrange("p (j e) -> p j e", e=2)[:, :, 1:2]
+        nc.vector.tensor_scalar(out=odd, in0=odd, scalar1=-1.0, scalar2=None, op0=ALU.mult)
         prm_ps = psum.tile([P, 4 * P], F32, name="prm_ps", tag="ps", bufs=PS_BUFS)
         nc.tensor.transpose(prm_ps[:, 0:P], prm_f[:], ident[:])
-        x_copies(0)
-        x_transposes(1)
+        copy_unit(1, shares(1))
         load_unit(7)
-        quant_unit(1)
         x_quant(0)
-        nc.vector.tensor_copy(out=prm[:], in_=prm_ps[:, 0:P])
-        copy_unit(2, shares(2))
-        load_unit(8)
         x_copies(1)
-        x_transposes(2)
-        load_unit(9)
-        quant_unit(2)
+        quant_unit(1)
         x_quant(1)
-        copy_unit(3, shares(3))
-        load_unit(10)
+        nc.vector.tensor_copy(out=prm[:], in_=prm_ps[:, 0:P])
+        nc.vector.tensor_scalar(out=prm[:, 64:96], in0=prm[:, 32:64], scalar1=prm[:, 96:97], scalar2=None, op0=ALU.mult)
+        x_transposes(2)
+        load_unit(8)
+        copy_unit(2, shares(2))
+        load_unit(9)
         x_copies(2)
+        quant_unit(2)
+        x_quant(2)
         x_transposes(3)
-        load_unit(11)
+        load_unit(10)
         tb_ps = []
         for i, tok_major in enumerate((cos_tok, sin_tok)):
             tb = psum.tile([P, TOK], F32, name="tb_ps", tag=("tb0", "tb1")[i], bufs=1)
@@ -232,10 +243,11 @@ def tile_causalselfattention_pa_kernel(tc, x, freqs, Wq, bq, Wk, bk, gq, gk, out
             for t in range(TT):
                 nc.tensor.transpose(tb[:, t * P : (t + 1) * P], tmv[:, t * P : (t + 1) * P], ident[:])
             tb_ps.append(tb)
-        quant_unit(3)
-        x_quant(2)
         x_copies(3)
+        copy_unit(3, shares(3))
+        load_unit(11)
         x_quant(3)
+        quant_unit(3)
         for u in range(4, 8):
             copy_unit(u, shares(u))
             load_unit(u + 8)
@@ -244,21 +256,26 @@ def tile_causalselfattention_pa_kernel(tc, x, freqs, Wq, bq, Wk, bk, gq, gk, out
         ssp = const.tile([P, 2, TT, NCHUNK], F32, name="ssp")
         rstd = const.tile([P, 2, TT], F32, name="rstd")
 
-        def mx_tile(s):
-            g, m = s // MT, s % MT
-            acc = psum.tile([P, TOK], F32, name="acc", tag="ps", bufs=PS_BUFS)
+        def mx_pair(s0):
+            g = s0 // MT
+            accs = []
+            for i in range(2):
+                acc = psum.tile([P, TOK], F32, name="acc", tag="ps", bufs=PS_BUFS)
+                accs.append(acc)
             for c in range(PASSES):
                 codes, scales = code_tiles[g * PASSES + c]
-                nc.tensor.matmul_mx(
-                    out=acc[:],
-                    lhsT=codes[:, m * P : (m + 1) * P].bitcast(E5X4),
-                    lhsT_scale=scales[:, m * P : (m + 1) * P],
-                    rhs=xcodes[:, c, :].bitcast(E5X4),
-                    rhs_scale=xscales[:, c, :],
-                    start=(c == 0),
-                    stop=(c == PASSES - 1),
-                )
-            return acc
+                for i in range(2):
+                    m = (s0 + i) % MT
+                    nc.tensor.matmul_mx(
+                        out=accs[i][:],
+                        lhsT=codes[:, m * P : (m + 1) * P].bitcast(E5X4),
+                        lhsT_scale=scales[:, m * P : (m + 1) * P],
+                        rhs=xcodes[:, c, :].bitcast(E5X4),
+                        rhs_scale=xscales[:, c, :],
+                        start=(c == 0),
+                        stop=(c == PASSES - 1),
+                    )
+            return accs
 
         def bias_tile(s, acc):
             a = work.tile([P, TOK], F32, name="a", tag="a", bufs=A_BUFS)
@@ -269,7 +286,7 @@ def tile_causalselfattention_pa_kernel(tc, x, freqs, Wq, bq, Wk, bk, gq, gk, out
             pr = work.tile([P, 2, TOK], F32, name="pr", tag="pr", bufs=PR_BUFS)
             for i in range(2):
                 nc.vector.scalar_tensor_tensor(
-                    out=pr[:, i, :], in0=a_tiles[s][:], scalar=prm[:, 32 + s : 33 + s], in1=tb_ps[i][:],
+                    out=pr[:, i, :], in0=a_tiles[s][:], scalar=prm[:, 32 * (i + 1) + s : 32 * (i + 1) + s + 1], in1=tb_ps[i][:],
                     op0=ALU.mult, op1=ALU.mult,
                 )
             p_tiles[s] = pr
@@ -283,7 +300,8 @@ def tile_causalselfattention_pa_kernel(tc, x, freqs, Wq, bq, Wk, bk, gq, gk, out
                     s = (NG - 1) * MT + m
                     for i in range(2):
                         nc.vector.scalar_tensor_tensor(
-                            out=p_tiles[s][:, i, cols], in0=a_tiles[s][:, cols], scalar=prm[:, 32 + s : 33 + s],
+                            out=p_tiles[s][:, i, cols], in0=a_tiles[s][:, cols],
+                            scalar=prm[:, 32 * (i + 1) + s : 32 * (i + 1) + s + 1],
                             in1=tb_ps[i][:, cols], op0=ALU.mult, op1=ALU.mult,
                         )
 
@@ -349,8 +367,7 @@ def tile_causalselfattention_pa_kernel(tc, x, freqs, Wq, bq, Wk, bk, gq, gk, out
             nc.sync.dma_start(out=outs[mat][t * P : (t + 1) * P, n0 : n0 + CHUNK], in_=st[:])
 
         for r in range(NROUND):
-            acc0 = mx_tile(2 * r)
-            acc1 = mx_tile(2 * r + 1)
+            acc0, acc1 = mx_pair(2 * r)
             if r == 0:
                 for u in range(4, 8):
                     quant_unit(u)
@@ -358,13 +375,13 @@ def tile_causalselfattention_pa_kernel(tc, x, freqs, Wq, bq, Wk, bk, gq, gk, out
                 quant_unit(2 * r + 4)
                 quant_unit(2 * r + 5)
             if r == TABLES_ROUND:
-                nc.vector.tensor_copy(out=tables[:, 0, :], in_=tb_ps[0][:])
-                nc.scalar.copy(out=tables[:, 1, :], in_=tb_ps[1][:])
+                nc.scalar.activation(out=tables[:, 1, :], in_=tb_ps[1][:], func=ACT.Copy, scale=prm[:, 96:97])
             if r == LAST_Q_ROUND:
                 for u in range(2 * r + 4, NUNIT):
                     quant_unit(u)
                 norm_mean(0)
                 norm_power(0)
+                nc.vector.tensor_copy(out=tables[:, 0, :], in_=tb_ps[0][:])
             for s in AG_IN.get(r, ()):
                 gain_tile(s)
             for s in TILES_IN.get(r, ()):

@@ -371,9 +371,9 @@ def tile_causalselfattention_pa_kernel(tc, x, freqs, Wq, bq, Wk, bk, gq, gk, out
             if r == 0:
                 for u in range(4, 8):
                     quant_unit(u)
-            if 2 <= r < LAST_Q_ROUND:
-                quant_unit(2 * r + 4)
-                quant_unit(2 * r + 5)
+            if 2 <= r < LAST_Q_ROUND and r % 2 == 0:
+                for u in range(2 * r + 4, 2 * r + 8):
+                    quant_unit(u)
             if r == TABLES_ROUND:
                 nc.scalar.activation(out=tables[:, 1, :], in_=tb_ps[1][:], func=ACT.Copy, scale=prm[:, 96:97])
             if r == LAST_Q_ROUND:

@@ -315,8 +315,7 @@ def tile_causalselfattention_pa_kernel(tc, x, freqs, Wq, bq, Wk, bk, gq, gk, out
         def rope_g(s):
             ag = ag_tiles[s]
             pr = work.tile([P, 2, TOK], F32, name="pr", tag="pr", bufs=PR_BUFS)
-            for i in range(2):
-                nc.gpsimd.tensor_tensor(out=pr[:, i, :], in0=ag[:], in1=tables[:, i, :], op=ALU.mult)
+            nc.gpsimd.tensor_tensor(out=pr[:], in0=ag[:].unsqueeze(1).to_broadcast([P, 2, TOK]), in1=tables[:], op=ALU.mult)
             p_tiles[s] = pr
 
         def rope(s):
@@ -412,7 +411,7 @@ def tile_causalselfattention_pa_kernel(tc, x, freqs, Wq, bq, Wk, bk, gq, gk, out
             elif g < NG:
                 for m in range(MT):
                     rope(g * MT + m)
-                    if g == 4 and m == 2:
+                    if g == 4 and m == 0:
                         norm_mean(1)
                     if g == 5 and m == 3:
                         norm_power(1)

from contextlib import ExitStack

import concourse.mybir as mybir
from concourse.masks import make_identity

F32 = mybir.dt.float32
BF16 = mybir.dt.bfloat16
U32 = mybir.dt.uint32
U8 = mybir.dt.uint8
E5X4 = mybir.dt.float8_e5m2_x4
ACT = mybir.ActivationFunctionType
ALU = mybir.AluOpType
AX = mybir.AxisListType

P = 128
TOK = 512
DIM = 2048
DQ = 2048
HP = 64
EPS = 1e-6
HALF_PI = 1.5707963267948966
K_PASS = 512
PASSES = DIM // K_PASS
TT = TOK // P
CHUNK = 512
NCHUNK = DQ // CHUNK
MT = CHUNK // P
NG = 2 * NCHUNK
NUNIT = NG * PASSES
NTILE = NG * MT
NROUND = NTILE // 2

FLOPS = 2 * TOK * DIM * 2 * DQ

def shares(u):
    if u < 4:
        return (304, 0)
    if u < 8:
        return (256, 0)
    if u < 12:
        return (352, 0)
    return (VC, 0)

VC = 448
A_BUFS = 32
PS_BUFS = 6
PR_BUFS = 16
ST_BUFS = 6
LAST_Q_ROUND = 12
TABLES_ROUND = 10
GT = (7, 11, 14, 15, 19, 23, 26, 27)
AG_IN = {12: (7,), 13: (11,), 14: (14, 15), 15: (19,)}
AG_IN2 = {3: (23,), 4: (26, 27)}
TILES_IN = {12: (0, 1), 13: (2, 3), 14: (4, 5, 6, 7), 15: (8, 9, 10, 11)}
UNITS_IN = {15: (0, 1, 2, 3)}
FV = (29, 31)


def tile_causalselfattention_pa_kernel(tc, x, freqs, Wq, bq, Wk, bk, gq, gk, out_0, out_1):
    nc = tc.nc
    weights = (Wq, Wk)
    outs = (out_0.rearrange("b t h d -> (b t) (h d)"), out_1.rearrange("b t h d -> (b t) (h d)"))

    with ExitStack() as ctx:
        ctx.enter_context(tc.manual_schedule(engines={mybir.EngineType.PE, mybir.EngineType.DVE, mybir.EngineType.Pool}))
        const = ctx.enter_context(tc.tile_pool(name="const", bufs=1))
        setup = ctx.enter_context(tc.tile_pool(name="setup", bufs=1))
        wpool = ctx.enter_context(tc.tile_pool(name="wpool", bufs=2))
        work = ctx.enter_context(tc.tile_pool(name="work", bufs=2))
        psum = ctx.enter_context(tc.psum_pool(name="psum", bufs=2))

        raw_tiles = {}
        wg_tiles = {}
        code_tiles = {}
        a_tiles = {}
        p_tiles = {}
        ta_tiles = {}
        to_tiles = {}

        def load_unit(u):
            g, c = u // PASSES, u % PASSES
            raw = wpool.tile([P, 4, CHUNK], BF16, name="raw", tag="raw", bufs=8)
            n0 = (g % NCHUNK) * CHUNK
            nc.sync.dma_start(
                out=raw[:],
                in_=weights[g // NCHUNK][c * K_PASS : (c + 1) * K_PASS, n0 : n0 + CHUNK].rearrange(
                    "(p j) w -> p j w", j=4
                ),
            )
            raw_tiles[u] = raw

        def copy_g(u, sh):
            wg = wpool.tile([P, CHUNK, 4], BF16, name="wg", tag="wg", bufs=4, align_bytes=64)
            wg_tiles[u] = wg
            g0 = CHUNK - sh[1]
            if sh[1] > 0:
                nc.gpsimd.tensor_scalar(
                    out=wg[:, g0:CHUNK, :], in0=raw_tiles[u][:, :, g0:CHUNK].rearrange("p t w -> p w t"),
                    scalar1=1.0, scalar2=0.0, op0=ALU.mult, op1=ALU.add,
                )

        def copy_vs(u, sh):
            wg = wg_tiles[u]
            raw = raw_tiles[u]
            vc = sh[0]
            g0 = CHUNK - sh[1]
            nc.vector.tensor_copy(
                out=wg[:, 0:vc, :].rearrange("p (c i) t -> p c t i", i=4),
                in_=raw[:, :, 0:vc].rearrange("p t (c i) -> p c t i", i=4),
            )
            nc.scalar.copy(
                out=wg[:, vc:g0, :].rearrange("p (c i) t -> p c t i", i=4),
                in_=raw[:, :, vc:g0].rearrange("p t (c i) -> p c t i", i=4),
            )

        def copy_unit(u, sh):
            copy_g(u, sh)
            copy_vs(u, sh)

        def quant_unit(u):
            codes = wpool.tile([P, CHUNK], U32, name="wcodes", tag="wcodes", bufs=8, align_bytes=64)
            scales = wpool.tile([P, CHUNK], U8, name="wscales", tag="wscales", bufs=8, align_bytes=64)
            nc.vector.quantize_mx(
                out=codes[:].bitcast(E5X4), scales=scales[:], in_=wg_tiles[u][:].rearrange("p w j -> p (w j)")
            )
            code_tiles[u] = (codes, scales)

        prm_raw = setup.tile([P, P], BF16, name="prm_raw")
        nc.vector.memset(prm_raw[:], 0.0)
        nc.vector.memset(prm_raw[96:P, :], 1.0)
        warm_in = setup.tile([P, 1], F32, name="warm_in")
        nc.vector.memset(warm_in[:], 1.0)
        minus_half = const.tile([P, TT], F32, name="minus_half")
        nc.vector.memset(minus_half[:], -0.5)
        fr_raw = setup.tile([P, TT, HP], BF16, name="fr_raw")
        nc.scalar.dma_start(out=fr_raw[:], in_=freqs.rearrange("(t p) j -> p t j", p=P))
        for v, vec in enumerate((bq, bk, gq, gk)):
            nc.scalar.dma_start(out=prm_raw[16 * v : 16 * v + 16, :], in_=vec.rearrange("(m p) -> m p", p=P))
        xv = x.rearrange("b (t p) k -> p (b t) k", p=P)
        xraw = {}

        def load_x(c):
            xr = wpool.tile([P, TT, K_PASS], BF16, name="xraw", tag="raw", bufs=8)
            nc.sync.dma_start(out=xr[:], in_=xv[:, :, c * K_PASS : (c + 1) * K_PASS])
            xraw[c] = xr

        load_unit(0)
        load_x(0)
        load_x(1)
        load_unit(1)
        load_x(2)
        load_unit(2)
        load_x(3)
        load_unit(3)

        ident = const.tile([P, P], F32, name="ident")
        make_identity(nc, ident[:])
        swap = const.tile([P, P], F32, name="swap")
        idv = ident[:].rearrange("p (j e) -> p j e", e=2)
        swv = swap[:].rearrange("p (j e) -> p j e", e=2)
        nc.vector.tensor_copy(out=swv[:, :, 0:1], in_=idv[:, :, 1:2])
        nc.vector.tensor_copy(out=swv[:, :, 1:2], in_=idv[:, :, 0:1])

        warm_out = setup.tile([P, 2], F32, name="warm_out")
        nc.scalar.activation(out=warm_out[:, 0:1], in_=warm_in[:], func=ACT.Sin)

        copy_unit(0, shares(0))
        load_unit(4)

        sin_tok = work.tile([P, TT, HP, 2], F32, name="sin_tok", tag="a", bufs=A_BUFS)
        nc.scalar.activation(out=sin_tok[:], in_=fr_raw[:].unsqueeze(3).to_broadcast([P, TT, HP, 2]), func=ACT.Sin)
        absf = work.tile([P, TT, HP], F32, name="absf", tag="a", bufs=A_BUFS)
        nc.scalar.activation(out=absf[:], in_=fr_raw[:], func=ACT.Abs)
        cos_tok = work.tile([P, TT, HP, 2], F32, name="cos_tok", tag="a", bufs=A_BUFS)
        nc.scalar.activation(
            out=cos_tok[:], in_=absf[:].unsqueeze(3).to_broadcast([P, TT, HP, 2]), func=ACT.Sin, scale=-1.0, bias=HALF_PI
        )

        xcodes = const.tile([P, PASSES, TOK], U32, name="xcodes", align_bytes=64)
        xscales = const.tile([P, PASSES, TOK], U8, name="xscales", align_bytes=64)
        xt_tiles = {}
        xg_tiles = {}

        def x_transposes(c):
            xw = xraw[c][:].bitcast(F32)
            for h in range(2):
                tag, bufs = "ps", PS_BUFS
                xt = psum.tile([P, 2, 2, P], F32, name="xt", tag=tag, bufs=bufs)
                for a in range(2):
                    for u in range(2):
                        nc.tensor.transpose(xt[:, a, u, :], xw[:, 2 * h + a, u : 256 : 2], ident[:])
                xt_tiles[(c, h)] = xt

        def x_copies(c):
            xg = wpool.tile([P, TOK * 4], BF16, name="xg", tag="wg", bufs=4, align_bytes=64)
            xgw = xg[:].bitcast(F32)
            for h in range(2):
                dst = xgw[:, 512 * h : 512 * (h + 1)].rearrange("p (a r u) -> p a r u", a=2, u=2)
                src = xt_tiles[(c, h)][:].rearrange("p a u r -> p a r u")
                if h == 0:
                    nc.vector.tensor_copy(out=dst, in_=src)
                else:
                    nc.scalar.copy(out=dst, in_=src)
            xg_tiles[c] = xg

        def x_quant(c):
            nc.vector.quantize_mx(out=xcodes[:, c, :].bitcast(E5X4), scales=xscales[:, c, :], in_=xg_tiles[c][:])

        prm = const.tile([P, P], F32, name="prm")
        x_transposes(0)
        load_unit(5)
        quant_unit(0)
        x_copies(0)
        x_transposes(1)
        load_unit(6)
        prm_f = setup.tile([P, P], F32, name="prm_f")
        nc.vector.tensor_copy(out=prm_f[:], in_=prm_raw[:])
        odd = prm_f[96:P, :].rearrange("p (j e) -> p j e", e=2)[:, :, 1:2]
        nc.vector.tensor_scalar(out=odd, in0=odd, scalar1=-1.0, scalar2=None, op0=ALU.mult)
        prm_ps = psum.tile([P, 4 * P], F32, name="prm_ps", tag="ps", bufs=PS_BUFS)
        nc.tensor.transpose(prm_ps[:, 0:P], prm_f[:], ident[:])
        copy_unit(1, shares(1))
        load_unit(7)
        x_quant(0)
        x_copies(1)
        quant_unit(1)
        x_quant(1)
        nc.vector.tensor_copy(out=prm[:], in_=prm_ps[:, 0:P])
        nc.vector.tensor_scalar(out=prm[:, 64:96], in0=prm[:, 32:64], scalar1=prm[:, 96:97], scalar2=None, op0=ALU.mult)
        x_transposes(2)
        load_unit(8)
        copy_unit(2, shares(2))
        load_unit(9)
        x_copies(2)
        quant_unit(2)
        x_quant(2)
        x_transposes(3)
        load_unit(10)
        tb_ps = []
        for i, tok_major in enumerate((cos_tok, sin_tok)):
            tb = psum.tile([P, TOK], F32, name="tb_ps", tag=("tb0", "tb1")[i], bufs=1)
            tmv = tok_major[:].rearrange("p t j e -> p (t j e)")
            for t in range(TT):
                nc.tensor.transpose(tb[:, t * P : (t + 1) * P], tmv[:, t * P : (t + 1) * P], ident[:])
            tb_ps.append(tb)
        x_copies(3)
        copy_unit(3, shares(3))
        load_unit(11)
        x_quant(3)
        quant_unit(3)
        for u in range(4, 8):
            copy_unit(u, shares(u))
            load_unit(u + 8)
        tables = const.tile([P, 2, TOK], F32, name="tables")

        ssp = const.tile([P, 2, TT, NCHUNK], F32, name="ssp")
        rstd = const.tile([P, 2, TT], F32, name="rstd")

        def mx_pair(s0):
            g = s0 // MT
            accs = []
            for i in range(2):
                acc = psum.tile([P, TOK], F32, name="acc", tag="ps", bufs=PS_BUFS)
                accs.append(acc)
            for c in range(PASSES):
                codes, scales = code_tiles[g * PASSES + c]
                for i in range(2):
                    m = (s0 + i) % MT
                    nc.tensor.matmul_mx(
                        out=accs[i][:],
                        lhsT=codes[:, m * P : (m + 1) * P].bitcast(E5X4),
                        lhsT_scale=scales[:, m * P : (m + 1) * P],
                        rhs=xcodes[:, c, :].bitcast(E5X4),
                        rhs_scale=xscales[:, c, :],
                        start=(c == 0),
                        stop=(c == PASSES - 1),
                    )
            return accs

        def bias_tile(s, acc):
            a = work.tile([P, TOK], F32, name="a", tag="a", bufs=A_BUFS)
            nc.scalar.activation(out=a[:], in_=acc[:], func=ACT.Identity, bias=prm[:, s : s + 1], scale=1.0)
            a_tiles[s] = a

        def rope_v(s):
            pr = work.tile([P, 2, TOK], F32, name="pr", tag="pr", bufs=PR_BUFS)
            for i in range(2):
                nc.vector.scalar_tensor_tensor(
                    out=pr[:, i, :], in0=a_tiles[s][:], scalar=prm[:, 32 * (i + 1) + s : 32 * (i + 1) + s + 1], in1=tb_ps[i][:],
                    op0=ALU.mult, op1=ALU.mult,
                )
            p_tiles[s] = pr

        def rope_last_chunk():
            for m in range(MT):
                p_tiles[(NG - 1) * MT + m] = work.tile([P, 2, TOK], F32, name="pr", tag="pr", bufs=PR_BUFS)
            for h in range(2):
                cols = slice(h * (TOK // 2), (h + 1) * (TOK // 2))
                for m in range(MT):
                    s = (NG - 1) * MT + m
                    for i in range(2):
                        nc.vector.scalar_tensor_tensor(
                            out=p_tiles[s][:, i, cols], in0=a_tiles[s][:, cols],
                            scalar=prm[:, 32 * (i + 1) + s : 32 * (i + 1) + s + 1],
                            in1=tb_ps[i][:, cols], op0=ALU.mult, op1=ALU.mult,
                        )

        ag_tiles = {}

        def gain_tile(s):
            ag = work.tile([P, TOK], F32, name="ag", tag="ag", bufs=8)
            nc.scalar.activation(out=ag[:], in_=a_tiles[s][:], func=ACT.Copy, scale=prm[:, 32 + s : 33 + s])
            ag_tiles[s] = ag

        def rope_g(s):
            ag = ag_tiles[s]
            pr = work.tile([P, 2, TOK], F32, name="pr", tag="pr", bufs=PR_BUFS)
            nc.gpsimd.tensor_tensor(out=pr[:], in0=ag[:].unsqueeze(1).to_broadcast([P, 2, TOK]), in1=tables[:], op=ALU.mult)
            p_tiles[s] = pr

        def rope(s):
            if s in GT:
                rope_g(s)
            else:
                rope_v(s)

        def sq_unit(g, t):
            ta = psum.tile([P, CHUNK], F32, name="ta", tag="ps", bufs=PS_BUFS)
            for m in range(MT):
                nc.tensor.transpose(ta[:, m * P : (m + 1) * P], a_tiles[g * MT + m][:, t * P : (t + 1) * P], ident[:])
            junk = work.tile([P, CHUNK], F32, name="junk", tag="junk", bufs=2)
            nc.scalar.activation(
                out=junk[:], in_=ta[:], func=ACT.Square,
                accum_out=ssp[:, g // NCHUNK, t, g % NCHUNK : g % NCHUNK + 1],
            )

        stat = const.tile([P, 2, 3, TT], F32, name="stat")

        def norm_mean(mat):
            nc.vector.tensor_reduce(out=stat[:, mat, 0, :], in_=ssp[:, mat, :, :], axis=AX.X, op=ALU.add)
            nc.vector.tensor_scalar(
                out=stat[:, mat, 1, :], in0=stat[:, mat, 0, :], scalar1=1.0 / DQ, scalar2=EPS, op0=ALU.mult, op1=ALU.add
            )

        def norm_power(mat):
            nc.gpsimd.tensor_tensor(out=rstd[:, mat, :], in0=stat[:, mat, 1, :], in1=minus_half[:], op=ALU.pow)

        def out_unit(j):
            g, t = j // TT, j % TT
            mat = g // NCHUNK
            to = psum.tile([P, CHUNK], F32, name="to", tag="ps", bufs=PS_BUFS)
            for m in range(MT):
                pr = p_tiles[g * MT + m]
                dst = to[:, m * P : (m + 1) * P]
                nc.tensor.matmul(dst, lhsT=pr[:, 0, t * P : (t + 1) * P], rhs=ident[:], is_transpose=True, start=True, stop=False)
                nc.tensor.matmul(dst, lhsT=pr[:, 1, t * P : (t + 1) * P], rhs=swap[:], is_transpose=True, start=False, stop=True)
            if j % 3 == 2:
                st = wpool.tile([P, CHUNK], F32, name="st", tag="wg", bufs=4, align_bytes=64)
            else:
                st = wpool.tile([P, CHUNK], F32, name="st", tag="raw", bufs=8)
            if j in FV:
                nc.vector.tensor_scalar(out=st[:], in0=to[:], scalar1=rstd[:, mat, t : t + 1], scalar2=None, op0=ALU.mult)
            else:
                nc.scalar.activation(out=st[:], in_=to[:], func=ACT.Copy, scale=rstd[:, mat, t : t + 1])
            n0 = (g % NCHUNK) * CHUNK
            nc.sync.dma_start(out=outs[mat][t * P : (t + 1) * P, n0 : n0 + CHUNK], in_=st[:])

        for r in range(NROUND):
            acc0, acc1 = mx_pair(2 * r)
            if r == 0:
                for u in range(4, 8):
                    quant_unit(u)
            if 2 <= r < LAST_Q_ROUND and r % 2 == 0:
                for u in range(2 * r + 4, 2 * r + 8):
                    quant_unit(u)
            if r == TABLES_ROUND:
                nc.scalar.activation(out=tables[:, 1, :], in_=tb_ps[1][:], func=ACT.Copy, scale=prm[:, 96:97])
            if r == LAST_Q_ROUND:
                for u in range(2 * r + 4, NUNIT):
                    quant_unit(u)
                norm_mean(0)
                norm_power(0)
                nc.vector.tensor_copy(out=tables[:, 0, :], in_=tb_ps[0][:])
            for s in AG_IN.get(r, ()):
                gain_tile(s)
            for s in TILES_IN.get(r, ()):
                rope(s)
            bias_tile(2 * r, acc0)
            bias_tile(2 * r + 1, acc1)
            if r >= 3 and r % 2 == 1:
                for t in range(TT):
                    sq_unit((r - 3) // 2, t)
            for j in UNITS_IN.get(r, ()):
                out_unit(j)
            if 2 * r + 9 < NUNIT:
                copy_unit(2 * r + 8, shares(2 * r + 8))
                copy_unit(2 * r + 9, shares(2 * r + 9))
            if 2 * r + 17 < NUNIT:
                load_unit(2 * r + 16)
                load_unit(2 * r + 17)

        for t in range(TT):
            sq_unit(NG - 1, t)
        for j in range(TT, 2 * TT):
            out_unit(j)
        for g in range(3, NG + 1):
            for s in AG_IN2.get(g, ()):
                gain_tile(s)
            if g == NG - 1:
                rope_last_chunk()
            elif g < NG:
                for m in range(MT):
                    rope(g * MT + m)
                    if g == 4 and m == 0:
                        norm_mean(1)
                    if g == 5 and m == 3:
                        norm_power(1)
            for t in range(TT):
                out_unit((g - 1) * TT + t)
